import numpy as np
import ml_dtypes


def mxq(x, axis, fmt="e4m3"):
    dtype, down = {"e4m3": (ml_dtypes.float8_e4m3fn, 7), "e5m2": (ml_dtypes.float8_e5m2, 14)}[fmt]
    v = np.moveaxis(np.asarray(x, np.float32).astype(ml_dtypes.bfloat16).astype(np.float64), axis, -1)
    blocks = v.reshape(v.shape[:-1] + (-1, 32))
    amax = np.abs(blocks).max(-1, keepdims=True)
    byte = np.maximum(np.where(amax > 0, np.frexp(amax)[1] - 1 + 127, 0) - down, 1)
    scale = np.exp2(byte - 127.0)
    codes = (blocks / scale).astype(np.float32).astype(dtype).astype(np.float64)
    return np.moveaxis((codes * scale).reshape(v.shape), -1, axis)


WIDE = False


def mx_kscale(k):
    if not WIDE:
        return np.ones(k)
    levels = np.array([10, -10, 5, -5, 0])
    a = np.random.permutation(np.resize(levels, k // 512 * 4)).reshape(k // 512, 4)
    idx = np.arange(k)
    return np.exp2(a[idx // 512, idx % 128 // 32])


BF16 = ml_dtypes.bfloat16


def bf(x):
    return np.asarray(x, np.float32).astype(BF16)


def f64(x):
    return np.asarray(x).astype(np.float64)


B, D, U = 4096, 256, 256
KD = 3 * U + D


def setup_inputs():
    s = np.ones(KD)
    s[3 * U:] = mx_kscale(KD)[:D]

    def gate():
        return bf(np.random.standard_normal((KD, U)) * 1.25 / np.sqrt(KD) / s[:, None])

    def bias():
        return bf(np.random.standard_normal(U) * 0.5)

    return {"x": bf(np.random.standard_normal((B, D)) * s[3 * U:]),
            "left_state": bf(np.random.standard_normal((B, U))),
            "top_state": bf(np.random.standard_normal((B, U))),
            "diagonal_state": bf(np.random.standard_normal((B, U))),
            "h_cand": bf(np.tanh(np.random.standard_normal((B, U)))),
            "w_zi": gate(), "b_zi": bias(), "w_zl": gate(), "b_zl": bias(),
            "w_zt": gate(), "b_zt": bias(), "w_zd": gate(), "b_zd": bias()}


def reference(x, left_state, top_state, diagonal_state, h_cand, w_zi, b_zi, w_zl, b_zl, w_zt, b_zt, w_zd, b_zd):
    left, top, diag = f64(left_state), f64(top_state), f64(diagonal_state)
    q = np.concatenate([left, top, diag, f64(x)], axis=1)
    W = np.concatenate([f64(w_zi), f64(w_zl), f64(w_zt), f64(w_zd)], axis=1)
    b = np.concatenate([f64(b_zi), f64(b_zl), f64(b_zt), f64(b_zd)])
    g = ((mxq(q, 1, "e4m3") @ mxq(W, 0, "e4m3")) + b).reshape(-1, 4, U)
    e = np.exp(g - g.max(axis=1, keepdims=True))
    z = e / e.sum(axis=1, keepdims=True)
    return z[:, 1] * left + z[:, 2] * top + z[:, 3] * diag + z[:, 0] * f64(h_cand)

@@ -1,0 +1,286 @@
+from contextlib import ExitStack
+
+import concourse.mybir as mybir
+from concourse.masks import make_identity
+
+F32 = mybir.dt.float32
+BF16 = mybir.dt.bfloat16
+U32 = mybir.dt.uint32
+U8 = mybir.dt.uint8
+FP8X4 = mybir.dt.float8_e4m3fn_x4
+ACT = mybir.ActivationFunctionType
+ALU = mybir.AluOpType
+
+P = 128
+BATCH = 4096
+UNITS = 256
+N_PAIRS = 16
+FLOPS = 2 * BATCH * 1024 * 1024
+
+
+def tile_multidimensinalgrucell_pb_t_kernel(
+    tc, x, left_state, top_state, diagonal_state, h_cand,
+    w_zi, b_zi, w_zl, b_zl, w_zt, b_zt, w_zd, b_zd, out,
+):
+    nc = tc.nc
+    gate_w = [w_zl, w_zt, w_zd, w_zi]
+    gate_b = [b_zl, b_zt, b_zd, b_zi]
+
+    def rows(a):
+        return a.rearrange("(p n t) f -> p n (t f)", n=N_PAIRS, t=2)
+
+    def rows3(a):
+        return a.rearrange("(p n t) f -> p n t f", n=N_PAIRS, t=2)
+
+    left_v, top_v, h_v, out_v = rows(left_state), rows(top_state), rows(h_cand), rows(out)
+    diag_v, x_v = rows3(diagonal_state), rows3(x)
+
+    with ExitStack() as ctx:
+        const = ctx.enter_context(tc.tile_pool(name="const", bufs=1))
+        inp = ctx.enter_context(tc.tile_pool(name="inp", bufs=3))
+        grp = ctx.enter_context(tc.tile_pool(name="grp", bufs=4))
+        qnt = ctx.enter_context(tc.tile_pool(name="qnt", bufs=2))
+        soft = ctx.enter_context(tc.tile_pool(name="soft", bufs=2))
+        fin = ctx.enter_context(tc.tile_pool(name="fin", bufs=2))
+        ps = ctx.enter_context(tc.psum_pool(name="ps", bufs=1))
+        ctx.enter_context(tc.manual_schedule())
+
+        st = {}
+
+        def load(n):
+            lf = inp.tile([P, 512], BF16, name="lf")
+            tp = inp.tile([P, 512], BF16, name="tp")
+            dx = inp.tile([P, 1024], BF16, name="dx")
+            hc = inp.tile([P, 512], BF16, name="hc")
+            dx4 = dx[:].rearrange("p (t s f) -> p t s f", t=2, s=2)
+            nc.sync.dma_start(out=lf[:], in_=left_v[:, n, :])
+            nc.sync.dma_start(out=tp[:], in_=top_v[:, n, :])
+            nc.sync.dma_start(out=dx4[:, :, 0, :], in_=diag_v[:, n])
+            nc.sync.dma_start(out=dx4[:, :, 1, :], in_=x_v[:, n])
+            nc.sync.dma_start(out=hc[:], in_=h_v[:, n, :])
+            st[("in", n)] = (lf, tp, dx, hc)
+
+        ident = const.tile([P, P], F32, name="ident")
+        make_identity(nc, ident[:])
+        brow = const.tile([P, 256], BF16, name="brow")
+        nc.vector.memset(brow[:], 0.0)
+        warm = const.tile([P, 8], F32, name="warm")
+        nc.vector.memset(warm[:], 0.0)
+        nc.scalar.activation(out=warm[:], in_=warm[:], func=ACT.Exp)
+        for j in range(4):
+            nc.scalar.dma_start(out=brow[j:j + 1, :], in_=gate_b[j].rearrange("(o f) -> o f", o=1))
+        load(0)
+        wraw = const.tile([P, 8192], BF16, name="wraw")
+        for j in range(4):
+            nc.sync.dma_start(
+                out=wraw[:, j * 2048:j * 2048 + 1024].rearrange("p (u y) -> p u y", u=2),
+                in_=gate_w[j][0:512, :].rearrange("(u p e) c -> p u (e c)", u=2, e=2),
+            )
+            nc.sync.dma_start(
+                out=wraw[:, j * 2048 + 1024:(j + 1) * 2048],
+                in_=gate_w[j][512:1024, :].rearrange("(p t) c -> p (t c)", t=4),
+            )
+        load(1)
+
+        tb0 = ps.tile([P, 256], F32, name="tb")
+        nc.tensor.transpose(tb0[:, 0:128], brow[:].bitcast(F32), ident[:])
+        bw = const.tile([P, 4], F32, name="bw")
+        nc.vector.tensor_copy(out=bw[:], in_=tb0[:, 0:4])
+        bcol = const.tile([P, 8], F32, name="bcol")
+        nc.vector.tensor_copy(out=bcol[:], in_=bw[:].bitcast(BF16))
+
+        wg = const.tile([P, 8192], BF16, name="wg", align_bytes=64)
+        wc = const.tile([P, 2048], U32, name="wc", align_bytes=64)
+        ws = const.tile([P, 2048], U8, name="ws", align_bytes=64)
+        wg6 = wg[:].rearrange("p (e s j c t) -> p e j s c t", e=2, s=2, j=4, t=4)
+
+        def regroup_w(eng_copy, eo, j):
+            src = wraw[:, j * 2048:(j + 1) * 2048].rearrange(
+                "p (s t c e) -> p e s c t", s=2, t=4, e=2)
+            eng_copy(out=wg6[:, eo, j], in_=src[:, eo])
+
+        def quant_w(eo):
+            nc.vector.quantize_mx(
+                out=wc[:, eo * 1024:(eo + 1) * 1024].bitcast(FP8X4),
+                scales=ws[:, eo * 1024:(eo + 1) * 1024],
+                in_=wg[:, eo * 4096:(eo + 1) * 4096],
+            )
+
+        for j in range(4):
+            regroup_w(nc.vector.tensor_copy, 0, j)
+        quant_w(0)
+
+        def in_t(n, tl):
+            lf, tp, dx, hc = st[("in", n)]
+            tr = ps.tile([P, 512], F32, name="tr")
+            tb = ps.tile([P, 256], F32, name="tb")
+            lfw, tpw, dxw, hcw = [a[:].bitcast(F32) for a in (lf, tp, dx, hc)]
+            w0 = tl * 128
+            d0 = tl * 256
+            nc.tensor.transpose(tr[:, 0:128], lfw[:, w0:w0 + 128], ident[:])
+            nc.tensor.transpose(tr[:, 128:256], tpw[:, w0:w0 + 128], ident[:])
+            nc.tensor.transpose(tr[:, 256:384], dxw[:, d0:d0 + 256:2], ident[:])
+            nc.tensor.transpose(tr[:, 384:512], dxw[:, d0 + 1:d0 + 256:2], ident[:])
+            nc.tensor.transpose(tb[:, 0:128], dxw[:, d0:d0 + 128], ident[:])
+            nc.tensor.transpose(tb[:, 128:256], hcw[:, w0:w0 + 128], ident[:])
+            st[("tr", n, tl)] = (tr, tb)
+
+        def evac(n, tl):
+            if tl == 0:
+                gq_new = grp.tile([P, 2048], BF16, name="gq", align_bytes=64)
+                gb_new = grp.tile([P, 1024], BF16, name="gb", align_bytes=64)
+                st[("g", n)] = (gq_new, gb_new)
+            gq, gb = st[("g", n)]
+            tr, tb = st[("tr", n, tl)]
+            c0 = tl * 128
+            nc.scalar.copy(
+                out=gq[:].bitcast(F32).rearrange("p (s c u) -> p s c u", s=2, u=2)[:, :, c0:c0 + 128, :],
+                in_=tr[:].rearrange("p (s u r) -> p s r u", s=2, u=2),
+            )
+            nc.scalar.copy(
+                out=gb[:].bitcast(F32).rearrange("p (c s) -> p c s", s=2)[:, c0:c0 + 128, :],
+                in_=tb[:].rearrange("p (s r) -> p r s", s=2),
+            )
+
+        def quant(n):
+            gq, gb = st[("g", n)]
+            qc = qnt.tile([P, 512], U32, name="qc", align_bytes=64)
+            qs = qnt.tile([P, 512], U8, name="qs", align_bytes=64)
+            nc.vector.quantize_mx(out=qc[:].bitcast(FP8X4), scales=qs[:], in_=gq[:])
+            st[("q", n)] = (qc, qs)
+
+        def mx(n):
+            qc, qs = st[("q", n)]
+            for eo in range(2):
+                la = ps.tile([P, 512], F32, name="la%d" % eo)
+                lb = ps.tile([P, 512], F32, name="lb%d" % eo)
+                st[("l", n, eo)] = (la, lb)
+                for j in range(4):
+                    bank = (la, lb)[j // 2]
+                    c0 = (j % 2) * 256
+                    for s in range(2):
+                        b0 = eo * 1024 + s * 512 + j * 128
+                        nc.tensor.matmul_mx(
+                            out=bank[:, c0:c0 + 256],
+                            lhsT=wc[:, b0:b0 + 128].bitcast(FP8X4),
+                            lhsT_scale=ws[:, b0:b0 + 128],
+                            rhs=qc[:, s * 256:(s + 1) * 256].bitcast(FP8X4),
+                            rhs_scale=qs[:, s * 256:(s + 1) * 256],
+                            start=(s == 0),
+                            stop=(s == 1),
+                        )
+
+        def logit(n, eo, j):
+            return st[("l", n, eo)][j // 2][:, (j % 2) * 256:(j % 2) * 256 + 256]
+
+        def bias(eo, j):
+            return bcol[:, 2 * j + eo:2 * j + eo + 1]
+
+        def first_gate(n):
+            for eo in range(2):
+                a0 = soft.tile([P, 256], F32, name="a0_%d" % eo)
+                nc.scalar.activation(out=a0[:], in_=logit(n, eo, 0), func=ACT.Identity,
+                                     bias=bias(eo, 0), scale=1.0)
+                st[("a0", n, eo)] = a0
+
+        def maxima(n):
+            for eo in range(2):
+                st[("m", n, eo)] = soft.tile([P, 256], F32, name="m_%d" % eo)
+            for j in range(1, 4):
+                for eo in range(2):
+                    m = st[("m", n, eo)]
+                    prev = st[("a0", n, eo)] if j == 1 else m
+                    nc.vector.scalar_tensor_tensor(
+                        out=m[:], in0=logit(n, eo, j), scalar=bias(eo, j), in1=prev[:],
+                        op0=ALU.add, op1=ALU.max)
+
+        def shifts(n):
+            for eo in range(2):
+                st[("e", n, eo)] = soft.tile([P, 1024], F32, name="e_%d" % eo)
+            for eo in range(2):
+                nc.gpsimd.tensor_tensor(out=st[("e", n, eo)][:, 0:256], in0=st[("a0", n, eo)][:],
+                                        in1=st[("m", n, eo)][:], op=ALU.subtract)
+            for eo in range(2):
+                for j in range(1, 4):
+                    nc.vector.scalar_tensor_tensor(
+                        out=st[("e", n, eo)][:, j * 256:(j + 1) * 256], in0=logit(n, eo, j),
+                        scalar=bias(eo, j), in1=st[("m", n, eo)][:],
+                        op0=ALU.add, op1=ALU.subtract)
+
+        def exps(n):
+            for eo in range(2):
+                e = st[("e", n, eo)]
+                nc.scalar.activation(out=e[:], in_=e[:], func=ACT.Exp)
+
+        def products(n):
+            gq, gb = st[("g", n)]
+            for eo in range(2):
+                e = st[("e", n, eo)]
+                pr = soft.tile([P, 1024], F32, name="pr_%d" % eo)
+                st[("pr", n, eo)] = pr
+                for half, src in ((0, gq[:, 0:1024]), (1, gb[:])):
+                    sv = src.rearrange("p (c u e) -> p u e c", u=2, e=2)[:, :, eo, :]
+                    nc.gpsimd.tensor_tensor(
+                        out=pr[:, half * 512:(half + 1) * 512].rearrange("p (u c) -> p u c", u=2),
+                        in0=e[:, half * 512:(half + 1) * 512].rearrange("p (u c) -> p u c", u=2),
+                        in1=sv, op=ALU.mult)
+
+        def out_t(n):
+            nd = [ps.tile([P, 512], F32, name="nd%d" % blk) for blk in range(2)]
+            st[("nd", n)] = nd
+            for kind, key in ((0, "e"), (1, "pr")):
+                for eo in range(2):
+                    src = st[(key, n, eo)]
+                    slot = kind * 2 + eo
+                    for blk in range(2):
+                        for j in range(4):
+                            nc.tensor.matmul(
+                                out=nd[blk][:, slot * 128:(slot + 1) * 128],
+                                lhsT=src[:, j * 256 + blk * 128:j * 256 + blk * 128 + 128],
+                                rhs=ident[:], is_transpose=True,
+                                start=(j == 0), stop=(j == 3))
+
+        def final(n):
+            nd = st[("nd", n)]
+            osb = fin.tile([P, 512], F32, name="osb")
+            rd = [fin.tile([P, 256], F32, name="rd%d" % blk) for blk in range(2)]
+            for blk in range(2):
+                nc.vector.reciprocal(out=rd[blk][:], in_=nd[blk][:, 0:256])
+            for blk in range(2):
+                nc.vector.tensor_tensor(
+                    out=osb[:, blk * 256:(blk + 1) * 256].rearrange("p (c e) -> p c e", e=2),
+                    in0=nd[blk][:, 256:512].rearrange("p (e c) -> p c e", e=2),
+                    in1=rd[blk][:].rearrange("p (e c) -> p c e", e=2),
+                    op=ALU.mult)
+            nc.sync.dma_start(out=out_v[:, n, :], in_=osb[:])
+
+        def ok(n):
+            return 0 <= n < N_PAIRS
+
+        for n in range(-2, N_PAIRS + 1):
+            if ok(n + 4):
+                load(n + 4)
+            if ok(n + 1):
+                evac(n + 1, 1)
+                quant(n + 1)
+            if n == -1:
+                for j in range(4):
+                    regroup_w(nc.scalar.copy, 1, j)
+                quant_w(1)
+            if ok(n):
+                mx(n)
+                first_gate(n)
+            if ok(n + 2):
+                in_t(n + 2, 0)
+                evac(n + 2, 0)
+            if ok(n):
+                maxima(n)
+                shifts(n)
+                exps(n)
+                products(n)
+            if ok(n - 1):
+                out_t(n - 1)
+            if ok(n + 2):
+                in_t(n + 2, 1)
+            if ok(n - 1):
+                final(n - 1)

@@ -37,7 +37,7 @@ def tile_multidimensinalgrucell_pb_t_kernel(
 
     with ExitStack() as ctx:
         const = ctx.enter_context(tc.tile_pool(name="const", bufs=1))
-        inp = ctx.enter_context(tc.tile_pool(name="inp", bufs=3))
+        inp = ctx.enter_context(tc.tile_pool(name="inp", bufs=4))
         grp = ctx.enter_context(tc.tile_pool(name="grp", bufs=4))
         qnt = ctx.enter_context(tc.tile_pool(name="qnt", bufs=2))
         soft = ctx.enter_context(tc.tile_pool(name="soft", bufs=2))
@@ -81,6 +81,8 @@ def tile_multidimensinalgrucell_pb_t_kernel(
                 in_=gate_w[j][512:1024, :].rearrange("(p t) c -> p (t c)", t=4),
             )
         load(1)
+        load(2)
+        load(3)
 
         tb0 = ps.tile([P, 256], F32, name="tb")
         nc.tensor.transpose(tb0[:, 0:128], brow[:].bitcast(F32), ident[:])
@@ -92,23 +94,19 @@ def tile_multidimensinalgrucell_pb_t_kernel(
         wg = const.tile([P, 8192], BF16, name="wg", align_bytes=64)
         wc = const.tile([P, 2048], U32, name="wc", align_bytes=64)
         ws = const.tile([P, 2048], U8, name="ws", align_bytes=64)
-        wg6 = wg[:].rearrange("p (e s j c t) -> p e j s c t", e=2, s=2, j=4, t=4)
+        wg6 = wg[:].rearrange("p (j e s c t) -> p j e s c t", j=4, e=2, s=2, t=4)
 
         def regroup_w(eng_copy, eo, j):
             src = wraw[:, j * 2048:(j + 1) * 2048].rearrange(
                 "p (s t c e) -> p e s c t", s=2, t=4, e=2)
-            eng_copy(out=wg6[:, eo, j], in_=src[:, eo])
+            eng_copy(out=wg6[:, j, eo], in_=src[:, eo])
 
-        def quant_w(eo):
+        def quant_w(j):
             nc.vector.quantize_mx(
-                out=wc[:, eo * 1024:(eo + 1) * 1024].bitcast(FP8X4),
-                scales=ws[:, eo * 1024:(eo + 1) * 1024],
-                in_=wg[:, eo * 4096:(eo + 1) * 4096],
+                out=wc[:, j * 512:(j + 1) * 512].bitcast(FP8X4),
+                scales=ws[:, j * 512:(j + 1) * 512],
+                in_=wg[:, j * 2048:(j + 1) * 2048],
             )
-
-        for j in range(4):
-            regroup_w(nc.vector.tensor_copy, 0, j)
-        quant_w(0)
 
         def in_t(n, tl):
             lf, tp, dx, hc = st[("in", n)]
@@ -159,7 +157,7 @@ def tile_multidimensinalgrucell_pb_t_kernel(
                     bank = (la, lb)[j // 2]
                     c0 = (j % 2) * 256
                     for s in range(2):
-                        b0 = eo * 1024 + s * 512 + j * 128
+                        b0 = j * 512 + eo * 256 + s * 128
                         nc.tensor.matmul_mx(
                             out=bank[:, c0:c0 + 256],
                             lhsT=wc[:, b0:b0 + 128].bitcast(FP8X4),
@@ -183,7 +181,7 @@ def tile_multidimensinalgrucell_pb_t_kernel(
                                      bias=bias(eo, 0), scale=1.0)
                 st[("a0", n, eo)] = a0
 
-        def maxima(n):
+        def maxima(n, fillers):
             for eo in range(2):
                 st[("m", n, eo)] = soft.tile([P, 256], F32, name="m_%d" % eo)
             for j in range(1, 4):
@@ -193,6 +191,9 @@ def tile_multidimensinalgrucell_pb_t_kernel(
                     nc.vector.scalar_tensor_tensor(
                         out=m[:], in0=logit(n, eo, j), scalar=bias(eo, j), in1=prev[:],
                         op0=ALU.add, op1=ALU.max)
+                    k = (j - 1) * 2 + eo
+                    if k < len(fillers):
+                        fillers[k]()
 
         def shifts(n):
             for eo in range(2):
@@ -212,75 +213,145 @@ def tile_multidimensinalgrucell_pb_t_kernel(
                 e = st[("e", n, eo)]
                 nc.scalar.activation(out=e[:], in_=e[:], func=ACT.Exp)
 
-        def products(n):
+        def products(n, eo, eng):
             gq, gb = st[("g", n)]
-            for eo in range(2):
-                e = st[("e", n, eo)]
-                pr = soft.tile([P, 1024], F32, name="pr_%d" % eo)
-                st[("pr", n, eo)] = pr
-                for half, src in ((0, gq[:, 0:1024]), (1, gb[:])):
-                    sv = src.rearrange("p (c u e) -> p u e c", u=2, e=2)[:, :, eo, :]
-                    nc.gpsimd.tensor_tensor(
-                        out=pr[:, half * 512:(half + 1) * 512].rearrange("p (u c) -> p u c", u=2),
-                        in0=e[:, half * 512:(half + 1) * 512].rearrange("p (u c) -> p u c", u=2),
-                        in1=sv, op=ALU.mult)
+            e = st[("e", n, eo)]
+            pr = soft.tile([P, 1024], F32, name="pr_%d" % eo)
+            st[("pr", n, eo)] = pr
+            for half, src in ((0, gq[:, 0:1024]), (1, gb[:])):
+                sv = src.rearrange("p (c u e) -> p u e c", u=2, e=2)[:, :, eo, :]
+                eng.tensor_tensor(
+                    out=pr[:, half * 512:(half + 1) * 512].rearrange("p (u c) -> p u c", u=2),
+                    in0=e[:, half * 512:(half + 1) * 512].rearrange("p (u c) -> p u c", u=2),
+                    in1=sv, op=ALU.mult)
 
         def out_t(n):
-            nd = [ps.tile([P, 512], F32, name="nd%d" % blk) for blk in range(2)]
-            st[("nd", n)] = nd
-            for kind, key in ((0, "e"), (1, "pr")):
+            den = ps.tile([P, 512], F32, name="den")
+            num = ps.tile([P, 512], F32, name="num")
+            st[("nd", n)] = (den, num)
+            for bank, key in ((den, "e"), (num, "pr")):
                 for eo in range(2):
                     src = st[(key, n, eo)]
-                    slot = kind * 2 + eo
                     for blk in range(2):
+                        c0 = blk * 256 + eo * 128
                         for j in range(4):
                             nc.tensor.matmul(
-                                out=nd[blk][:, slot * 128:(slot + 1) * 128],
+                                out=bank[:, c0:c0 + 128],
                                 lhsT=src[:, j * 256 + blk * 128:j * 256 + blk * 128 + 128],
                                 rhs=ident[:], is_transpose=True,
                                 start=(j == 0), stop=(j == 3))
 
-        def final(n):
-            nd = st[("nd", n)]
+        def bec(ap):
+            return ap.rearrange("p (b e c) -> p b e c", b=2, e=2)
+
+        def swap_den(n):
+            den, num = st[("nd", n)]
+            dsw = fin.tile([P, 512], F32, name="dsw")
+            st[("dsw", n)] = dsw
+            for eo in range(2):
+                nc.scalar.copy(out=bec(dsw[:])[:, :, eo, :], in_=bec(den[:])[:, :, 1 - eo, :])
+
+        def div_p(n):
+            den, num = st[("nd", n)]
+            dsw = st[("dsw", n)]
+            pp = fin.tile([P, 256], F32, name="pp")
+            cr = fin.tile([P, 512], F32, name="cr")
+            st[("div", n)] = (pp, cr)
+            nc.vector.tensor_tensor(out=pp[:].rearrange("p (b c) -> p b c", b=2),
+                                    in0=bec(den[:])[:, :, 0, :], in1=bec(dsw[:])[:, :, 0, :],
+                                    op=ALU.mult)
+            nc.vector.tensor_tensor(out=cr[:], in0=num[:], in1=dsw[:], op=ALU.mult)
+
+        def div_q(n):
+            pp, cr = st[("div", n)]
+            qq = fin.tile([P, 128], F32, name="qq")
+            st[("qq", n)] = qq
+            nc.vector.tensor_tensor(out=qq[:], in0=pp[:, 0:128], in1=pp[:, 128:256], op=ALU.mult)
+
+        def div_r(n):
+            rr = fin.tile([P, 128], F32, name="rr")
+            st[("rr", n)] = rr
+            nc.vector.reciprocal(out=rr[:], in_=st[("qq", n)][:])
+
+        def div_s(n):
+            pp, cr = st[("div", n)]
+            sb = fin.tile([P, 256], F32, name="sb")
+            st[("sb", n)] = sb
+            for blk in range(2):
+                nc.vector.tensor_tensor(out=sb[:, blk * 128:(blk + 1) * 128], in0=st[("rr", n)][:],
+                                        in1=pp[:, (1 - blk) * 128:(2 - blk) * 128], op=ALU.mult)
+
+        def div_out(n):
+            pp, cr = st[("div", n)]
             osb = fin.tile([P, 512], F32, name="osb")
-            rd = [fin.tile([P, 256], F32, name="rd%d" % blk) for blk in range(2)]
-            for blk in range(2):
-                nc.vector.reciprocal(out=rd[blk][:], in_=nd[blk][:, 0:256])
-            for blk in range(2):
-                nc.vector.tensor_tensor(
-                    out=osb[:, blk * 256:(blk + 1) * 256].rearrange("p (c e) -> p c e", e=2),
-                    in0=nd[blk][:, 256:512].rearrange("p (e c) -> p c e", e=2),
-                    in1=rd[blk][:].rearrange("p (e c) -> p c e", e=2),
-                    op=ALU.mult)
+            nc.vector.tensor_tensor(
+                out=osb[:].rearrange("p (b c e) -> p b c e", b=2, e=2),
+                in0=cr[:].rearrange("p (b e c) -> p b c e", b=2, e=2),
+                in1=st[("sb", n)][:].rearrange("p (b c) -> p b c", b=2).unsqueeze(3).to_broadcast([P, 2, 128, 2]),
+                op=ALU.mult)
             nc.sync.dma_start(out=out_v[:, n, :], in_=osb[:])
 
         def ok(n):
             return 0 <= n < N_PAIRS
 
-        for n in range(-2, N_PAIRS + 1):
+        in_t(0, 0)
+        evac(0, 0)
+        in_t(0, 1)
+        for j in range(4):
+            regroup_w(nc.vector.tensor_copy, 0, j)
+            regroup_w(nc.scalar.copy, 1, j)
+            if j == 0:
+                evac(0, 1)
+            else:
+                quant_w(j - 1)
+        quant(0)
+        quant_w(3)
+
+        last = N_PAIRS - 1
+        for n in range(0, N_PAIRS + 2):
             if ok(n + 4):
                 load(n + 4)
-            if ok(n + 1):
+            if n > 0 and ok(n + 1):
                 evac(n + 1, 1)
+            if ok(n - 2):
+                div_q(n - 2)
+            if n > 0 and ok(n + 1):
                 quant(n + 1)
-            if n == -1:
-                for j in range(4):
-                    regroup_w(nc.scalar.copy, 1, j)
-                quant_w(1)
+            if ok(n - 2):
+                div_r(n - 2)
             if ok(n):
                 mx(n)
                 first_gate(n)
+            if n == 0:
+                in_t(1, 0)
+                evac(1, 0)
+                in_t(1, 1)
+                evac(1, 1)
             if ok(n + 2):
                 in_t(n + 2, 0)
                 evac(n + 2, 0)
+            fillers = []
+            if ok(n - 2):
+                fillers = [lambda: div_s(n - 2), lambda: div_out(n - 2)]
             if ok(n):
-                maxima(n)
+                maxima(n, fillers)
                 shifts(n)
-                exps(n)
-                products(n)
+            else:
+                for f in fillers:
+                    f()
+            if n == 0:
+                quant(1)
             if ok(n - 1):
                 out_t(n - 1)
+                swap_den(n - 1)
+            if ok(n):
+                exps(n)
+                products(n, 0, nc.gpsimd)
+                if n < last:
+                    products(n, 1, nc.gpsimd)
             if ok(n + 2):
                 in_t(n + 2, 1)
             if ok(n - 1):
-                final(n - 1)
+                div_p(n - 1)
+            if n == last:
+                products(n, 1, nc.vector)

@@ -181,7 +181,7 @@ def tile_multidimensinalgrucell_pb_t_kernel(
                                      bias=bias(eo, 0), scale=1.0)
                 st[("a0", n, eo)] = a0
 
-        def maxima(n, fillers):
+        def maxima(n):
             for eo in range(2):
                 st[("m", n, eo)] = soft.tile([P, 256], F32, name="m_%d" % eo)
             for j in range(1, 4):
@@ -191,9 +191,6 @@ def tile_multidimensinalgrucell_pb_t_kernel(
                     nc.vector.scalar_tensor_tensor(
                         out=m[:], in0=logit(n, eo, j), scalar=bias(eo, j), in1=prev[:],
                         op0=ALU.add, op1=ALU.max)
-                    k = (j - 1) * 2 + eo
-                    if k < len(fillers):
-                        fillers[k]()
 
         def shifts(n):
             for eo in range(2):
@@ -262,32 +259,19 @@ def tile_multidimensinalgrucell_pb_t_kernel(
                                     op=ALU.mult)
             nc.vector.tensor_tensor(out=cr[:], in0=num[:], in1=dsw[:], op=ALU.mult)
 
-        def div_q(n):
-            pp, cr = st[("div", n)]
-            qq = fin.tile([P, 128], F32, name="qq")
-            st[("qq", n)] = qq
-            nc.vector.tensor_tensor(out=qq[:], in0=pp[:, 0:128], in1=pp[:, 128:256], op=ALU.mult)
-
         def div_r(n):
-            rr = fin.tile([P, 128], F32, name="rr")
-            st[("rr", n)] = rr
-            nc.vector.reciprocal(out=rr[:], in_=st[("qq", n)][:])
-
-        def div_s(n):
             pp, cr = st[("div", n)]
-            sb = fin.tile([P, 256], F32, name="sb")
-            st[("sb", n)] = sb
-            for blk in range(2):
-                nc.vector.tensor_tensor(out=sb[:, blk * 128:(blk + 1) * 128], in0=st[("rr", n)][:],
-                                        in1=pp[:, (1 - blk) * 128:(2 - blk) * 128], op=ALU.mult)
+            rr = fin.tile([P, 256], F32, name="rr")
+            st[("rr", n)] = rr
+            nc.vector.reciprocal(out=rr[:], in_=pp[:])
 
         def div_out(n):
             pp, cr = st[("div", n)]
             osb = fin.tile([P, 512], F32, name="osb")
-            nc.vector.tensor_tensor(
+            nc.gpsimd.tensor_tensor(
                 out=osb[:].rearrange("p (b c e) -> p b c e", b=2, e=2),
                 in0=cr[:].rearrange("p (b e c) -> p b c e", b=2, e=2),
-                in1=st[("sb", n)][:].rearrange("p (b c) -> p b c", b=2).unsqueeze(3).to_broadcast([P, 2, 128, 2]),
+                in1=st[("rr", n)][:].rearrange("p (b c) -> p b c", b=2).unsqueeze(3).to_broadcast([P, 2, 128, 2]),
                 op=ALU.mult)
             nc.sync.dma_start(out=out_v[:, n, :], in_=osb[:])
 
@@ -313,12 +297,11 @@ def tile_multidimensinalgrucell_pb_t_kernel(
                 load(n + 4)
             if n > 0 and ok(n + 1):
                 evac(n + 1, 1)
-            if ok(n - 2):
-                div_q(n - 2)
             if n > 0 and ok(n + 1):
                 quant(n + 1)
             if ok(n - 2):
                 div_r(n - 2)
+                div_out(n - 2)
             if ok(n):
                 mx(n)
                 first_gate(n)
@@ -330,15 +313,9 @@ def tile_multidimensinalgrucell_pb_t_kernel(
             if ok(n + 2):
                 in_t(n + 2, 0)
                 evac(n + 2, 0)
-            fillers = []
-            if ok(n - 2):
-                fillers = [lambda: div_s(n - 2), lambda: div_out(n - 2)]
             if ok(n):
-                maxima(n, fillers)
+                maxima(n)
                 shifts(n)
-            else:
-                for f in fillers:
-                    f()
             if n == 0:
                 quant(1)
             if ok(n - 1):

@@ -194,14 +194,11 @@ def tile_multidimensinalgrucell_pb_t_kernel(
 
         def shifts(n):
             for eo in range(2):
-                st[("e", n, eo)] = soft.tile([P, 1024], F32, name="e_%d" % eo)
-            for eo in range(2):
-                nc.gpsimd.tensor_tensor(out=st[("e", n, eo)][:, 0:256], in0=st[("a0", n, eo)][:],
-                                        in1=st[("m", n, eo)][:], op=ALU.subtract)
-            for eo in range(2):
-                for j in range(1, 4):
+                e = soft.tile([P, 1024], F32, name="e_%d" % eo)
+                st[("e", n, eo)] = e
+                for j in range(4):
                     nc.vector.scalar_tensor_tensor(
-                        out=st[("e", n, eo)][:, j * 256:(j + 1) * 256], in0=logit(n, eo, j),
+                        out=e[:, j * 256:(j + 1) * 256], in0=logit(n, eo, j),
                         scalar=bias(eo, j), in1=st[("m", n, eo)][:],
                         op0=ALU.add, op1=ALU.subtract)
 
@@ -248,27 +245,30 @@ def tile_multidimensinalgrucell_pb_t_kernel(
             for eo in range(2):
                 nc.scalar.copy(out=bec(dsw[:])[:, :, eo, :], in_=bec(den[:])[:, :, 1 - eo, :])
 
-        def div_p(n):
+        def div_pp(n):
             den, num = st[("nd", n)]
-            dsw = st[("dsw", n)]
             pp = fin.tile([P, 256], F32, name="pp")
-            cr = fin.tile([P, 512], F32, name="cr")
-            st[("div", n)] = (pp, cr)
+            st[("pp", n)] = pp
             nc.vector.tensor_tensor(out=pp[:].rearrange("p (b c) -> p b c", b=2),
-                                    in0=bec(den[:])[:, :, 0, :], in1=bec(dsw[:])[:, :, 0, :],
+                                    in0=bec(den[:])[:, :, 0, :], in1=bec(st[("dsw", n)][:])[:, :, 0, :],
                                     op=ALU.mult)
-            nc.vector.tensor_tensor(out=cr[:], in0=num[:], in1=dsw[:], op=ALU.mult)
+
+        def div_cr(n):
+            den, num = st[("nd", n)]
+            cr = fin.tile([P, 512], F32, name="cr")
+            st[("cr", n)] = cr
+            nc.vector.tensor_tensor(out=cr[:], in0=num[:], in1=st[("dsw", n)][:], op=ALU.mult)
 
         def div_r(n):
-            pp, cr = st[("div", n)]
+            pp = st[("pp", n)]
             rr = fin.tile([P, 256], F32, name="rr")
             st[("rr", n)] = rr
             nc.vector.reciprocal(out=rr[:], in_=pp[:])
 
-        def div_out(n):
-            pp, cr = st[("div", n)]
+        def div_out(n, eng):
+            cr = st[("cr", n)]
             osb = fin.tile([P, 512], F32, name="osb")
-            nc.gpsimd.tensor_tensor(
+            eng.tensor_tensor(
                 out=osb[:].rearrange("p (b c e) -> p b c e", b=2, e=2),
                 in0=cr[:].rearrange("p (b e c) -> p b c e", b=2, e=2),
                 in1=st[("rr", n)][:].rearrange("p (b c) -> p b c", b=2).unsqueeze(3).to_broadcast([P, 2, 128, 2]),
@@ -292,16 +292,9 @@ def tile_multidimensinalgrucell_pb_t_kernel(
         quant_w(3)
 
         last = N_PAIRS - 1
-        for n in range(0, N_PAIRS + 2):
+        for n in range(0, N_PAIRS + 1):
             if ok(n + 4):
                 load(n + 4)
-            if n > 0 and ok(n + 1):
-                evac(n + 1, 1)
-            if n > 0 and ok(n + 1):
-                quant(n + 1)
-            if ok(n - 2):
-                div_r(n - 2)
-                div_out(n - 2)
             if ok(n):
                 mx(n)
                 first_gate(n)
@@ -310,9 +303,13 @@ def tile_multidimensinalgrucell_pb_t_kernel(
                 evac(1, 0)
                 in_t(1, 1)
                 evac(1, 1)
+            elif ok(n + 1):
+                evac(n + 1, 1)
             if ok(n + 2):
                 in_t(n + 2, 0)
                 evac(n + 2, 0)
+            if n > 0 and ok(n + 1):
+                quant(n + 1)
             if ok(n):
                 maxima(n)
                 shifts(n)
@@ -328,7 +325,15 @@ def tile_multidimensinalgrucell_pb_t_kernel(
                     products(n, 1, nc.gpsimd)
             if ok(n + 2):
                 in_t(n + 2, 1)
-            if ok(n - 1):
-                div_p(n - 1)
+            if ok(n - 1) and n - 1 < last:
+                div_pp(n - 1)
+                div_cr(n - 1)
+                div_r(n - 1)
+                div_out(n - 1, nc.gpsimd)
             if n == last:
                 products(n, 1, nc.vector)
+            if n - 1 == last:
+                div_pp(last)
+                div_r(last)
+                div_cr(last)
+                div_out(last, nc.vector)

@@ -295,6 +295,9 @@ def tile_multidimensinalgrucell_pb_t_kernel(
         for n in range(0, N_PAIRS + 1):
             if ok(n + 4):
                 load(n + 4)
+            if n > 0 and ok(n + 1):
+                evac(n + 1, 1)
+                quant(n + 1)
             if ok(n):
                 mx(n)
                 first_gate(n)
@@ -303,13 +306,9 @@ def tile_multidimensinalgrucell_pb_t_kernel(
                 evac(1, 0)
                 in_t(1, 1)
                 evac(1, 1)
-            elif ok(n + 1):
-                evac(n + 1, 1)
             if ok(n + 2):
                 in_t(n + 2, 0)
                 evac(n + 2, 0)
-            if n > 0 and ok(n + 1):
-                quant(n + 1)
             if ok(n):
                 maxima(n)
                 shifts(n)

@@ -15,6 +15,7 @@ P = 128
 BATCH = 4096
 UNITS = 256
 N_PAIRS = 16
+HALVES = 2 * N_PAIRS
 FLOPS = 2 * BATCH * 1024 * 1024
 
 
@@ -37,12 +38,13 @@ def tile_multidimensinalgrucell_pb_t_kernel(
 
     with ExitStack() as ctx:
         const = ctx.enter_context(tc.tile_pool(name="const", bufs=1))
-        inp = ctx.enter_context(tc.tile_pool(name="inp", bufs=4))
-        grp = ctx.enter_context(tc.tile_pool(name="grp", bufs=4))
+        inp = ctx.enter_context(tc.tile_pool(name="inp", bufs=6))
+        grp = ctx.enter_context(tc.tile_pool(name="grp", bufs=5))
         qnt = ctx.enter_context(tc.tile_pool(name="qnt", bufs=2))
-        soft = ctx.enter_context(tc.tile_pool(name="soft", bufs=2))
-        fin = ctx.enter_context(tc.tile_pool(name="fin", bufs=2))
+        soft = ctx.enter_context(tc.tile_pool(name="soft", bufs=3))
+        fin = ctx.enter_context(tc.tile_pool(name="fin", bufs=3))
         ps = ctx.enter_context(tc.psum_pool(name="ps", bufs=1))
+        ps2 = ctx.enter_context(tc.psum_pool(name="ps2", bufs=2))
         ctx.enter_context(tc.manual_schedule())
 
         st = {}
@@ -83,8 +85,9 @@ def tile_multidimensinalgrucell_pb_t_kernel(
         load(1)
         load(2)
         load(3)
+        load(4)
 
-        tb0 = ps.tile([P, 256], F32, name="tb")
+        tb0 = ps2.tile([P, 512], F32, name="tr")
         nc.tensor.transpose(tb0[:, 0:128], brow[:].bitcast(F32), ident[:])
         bw = const.tile([P, 4], F32, name="bw")
         nc.vector.tensor_copy(out=bw[:], in_=tb0[:, 0:4])
@@ -94,183 +97,189 @@ def tile_multidimensinalgrucell_pb_t_kernel(
         wg = const.tile([P, 8192], BF16, name="wg", align_bytes=64)
         wc = const.tile([P, 2048], U32, name="wc", align_bytes=64)
         ws = const.tile([P, 2048], U8, name="ws", align_bytes=64)
-        wg6 = wg[:].rearrange("p (j e s c t) -> p j e s c t", j=4, e=2, s=2, t=4)
+        wg6 = wg[:].rearrange("p (e j s c t) -> p e j s c t", e=2, j=4, s=2, t=4)
 
         def regroup_w(eng_copy, eo, j):
             src = wraw[:, j * 2048:(j + 1) * 2048].rearrange(
                 "p (s t c e) -> p e s c t", s=2, t=4, e=2)
-            eng_copy(out=wg6[:, j, eo], in_=src[:, eo])
+            eng_copy(out=wg6[:, eo, j], in_=src[:, eo])
 
-        def quant_w(j):
+        def quant_w(eo, jp):
+            g0 = eo * 4 + jp * 2
             nc.vector.quantize_mx(
-                out=wc[:, j * 512:(j + 1) * 512].bitcast(FP8X4),
-                scales=ws[:, j * 512:(j + 1) * 512],
-                in_=wg[:, j * 2048:(j + 1) * 2048],
+                out=wc[:, g0 * 256:(g0 + 2) * 256].bitcast(FP8X4),
+                scales=ws[:, g0 * 256:(g0 + 2) * 256],
+                in_=wg[:, g0 * 1024:(g0 + 2) * 1024],
             )
 
-        def in_t(n, tl):
+        def in_q(n, tl):
             lf, tp, dx, hc = st[("in", n)]
-            tr = ps.tile([P, 512], F32, name="tr")
-            tb = ps.tile([P, 256], F32, name="tb")
-            lfw, tpw, dxw, hcw = [a[:].bitcast(F32) for a in (lf, tp, dx, hc)]
+            tr = ps2.tile([P, 512], F32, name="tr")
+            lfw, tpw, dxw = [a[:].bitcast(F32) for a in (lf, tp, dx)]
             w0 = tl * 128
             d0 = tl * 256
             nc.tensor.transpose(tr[:, 0:128], lfw[:, w0:w0 + 128], ident[:])
             nc.tensor.transpose(tr[:, 128:256], tpw[:, w0:w0 + 128], ident[:])
             nc.tensor.transpose(tr[:, 256:384], dxw[:, d0:d0 + 256:2], ident[:])
             nc.tensor.transpose(tr[:, 384:512], dxw[:, d0 + 1:d0 + 256:2], ident[:])
-            nc.tensor.transpose(tb[:, 0:128], dxw[:, d0:d0 + 128], ident[:])
-            nc.tensor.transpose(tb[:, 128:256], hcw[:, w0:w0 + 128], ident[:])
-            st[("tr", n, tl)] = (tr, tb)
+            st[("tr", n, tl)] = tr
 
-        def evac(n, tl):
+        def evac_q(n, tl):
             if tl == 0:
                 gq_new = grp.tile([P, 2048], BF16, name="gq", align_bytes=64)
-                gb_new = grp.tile([P, 1024], BF16, name="gb", align_bytes=64)
-                st[("g", n)] = (gq_new, gb_new)
-            gq, gb = st[("g", n)]
-            tr, tb = st[("tr", n, tl)]
+                st[("gq", n)] = gq_new
             c0 = tl * 128
             nc.scalar.copy(
-                out=gq[:].bitcast(F32).rearrange("p (s c u) -> p s c u", s=2, u=2)[:, :, c0:c0 + 128, :],
-                in_=tr[:].rearrange("p (s u r) -> p s r u", s=2, u=2),
+                out=st[("gq", n)][:].bitcast(F32).rearrange("p (s c u) -> p s c u", s=2, u=2)[:, :, c0:c0 + 128, :],
+                in_=st[("tr", n, tl)][:].rearrange("p (s u r) -> p s r u", s=2, u=2),
             )
+
+        def in_b(n):
+            lf, tp, dx, hc = st[("in", n)]
+            tb = ps2.tile([P, 512], F32, name="tr")
+            dxw, hcw = [a[:].bitcast(F32) for a in (dx, hc)]
+            for tl in range(2):
+                nc.tensor.transpose(tb[:, tl * 128:tl * 128 + 128], dxw[:, tl * 256:tl * 256 + 128], ident[:])
+            for tl in range(2):
+                nc.tensor.transpose(tb[:, 256 + tl * 128:384 + tl * 128], hcw[:, tl * 128:tl * 128 + 128], ident[:])
+            st[("tb", n)] = tb
+
+        def evac_b(n):
+            gb = grp.tile([P, 1024], BF16, name="gb", align_bytes=64)
+            st[("gb", n)] = gb
             nc.scalar.copy(
-                out=gb[:].bitcast(F32).rearrange("p (c s) -> p c s", s=2)[:, c0:c0 + 128, :],
-                in_=tb[:].rearrange("p (s r) -> p r s", s=2),
+                out=gb[:].bitcast(F32).rearrange("p (c s) -> p c s", s=2),
+                in_=st[("tb", n)][:].rearrange("p (s c) -> p c s", s=2),
             )
 
-        def quant(n):
-            gq, gb = st[("g", n)]
-            qc = qnt.tile([P, 512], U32, name="qc", align_bytes=64)
-            qs = qnt.tile([P, 512], U8, name="qs", align_bytes=64)
-            nc.vector.quantize_mx(out=qc[:].bitcast(FP8X4), scales=qs[:], in_=gq[:])
-            st[("q", n)] = (qc, qs)
-
-        def mx(n):
+        def quant(n, s):
+            if s == 0:
+                qc_new = qnt.tile([P, 512], U32, name="qc", align_bytes=64)
+                qs_new = qnt.tile([P, 512], U8, name="qs", align_bytes=64)
+                st[("q", n)] = (qc_new, qs_new)
             qc, qs = st[("q", n)]
-            for eo in range(2):
-                la = ps.tile([P, 512], F32, name="la%d" % eo)
-                lb = ps.tile([P, 512], F32, name="lb%d" % eo)
-                st[("l", n, eo)] = (la, lb)
-                for j in range(4):
-                    bank = (la, lb)[j // 2]
-                    c0 = (j % 2) * 256
-                    for s in range(2):
-                        b0 = j * 512 + eo * 256 + s * 128
-                        nc.tensor.matmul_mx(
-                            out=bank[:, c0:c0 + 256],
-                            lhsT=wc[:, b0:b0 + 128].bitcast(FP8X4),
-                            lhsT_scale=ws[:, b0:b0 + 128],
-                            rhs=qc[:, s * 256:(s + 1) * 256].bitcast(FP8X4),
-                            rhs_scale=qs[:, s * 256:(s + 1) * 256],
-                            start=(s == 0),
-                            stop=(s == 1),
-                        )
+            nc.vector.quantize_mx(
+                out=qc[:, s * 256:(s + 1) * 256].bitcast(FP8X4),
+                scales=qs[:, s * 256:(s + 1) * 256],
+                in_=st[("gq", n)][:, s * 1024:(s + 1) * 1024])
 
-        def logit(n, eo, j):
-            return st[("l", n, eo)][j // 2][:, (j % 2) * 256:(j % 2) * 256 + 256]
+        def mx(h):
+            n, eo = divmod(h, 2)
+            qc, qs = st[("q", n)]
+            la = ps.tile([P, 512], F32, name="la%d" % eo)
+            lb = ps.tile([P, 512], F32, name="lb%d" % eo)
+            st[("l", h)] = (la, lb)
+            for j in range(4):
+                bank = (la, lb)[j // 2]
+                c0 = (j % 2) * 256
+                for s in range(2):
+                    b0 = ((eo * 4 + j) * 2 + s) * 128
+                    nc.tensor.matmul_mx(
+                        out=bank[:, c0:c0 + 256],
+                        lhsT=wc[:, b0:b0 + 128].bitcast(FP8X4),
+                        lhsT_scale=ws[:, b0:b0 + 128],
+                        rhs=qc[:, s * 256:(s + 1) * 256].bitcast(FP8X4),
+                        rhs_scale=qs[:, s * 256:(s + 1) * 256],
+                        start=(s == 0),
+                        stop=(s == 1),
+                    )
 
-        def bias(eo, j):
-            return bcol[:, 2 * j + eo:2 * j + eo + 1]
+        def logit(h, j):
+            return st[("l", h)][j // 2][:, (j % 2) * 256:(j % 2) * 256 + 256]
 
-        def first_gate(n):
-            for eo in range(2):
-                a0 = soft.tile([P, 256], F32, name="a0_%d" % eo)
-                nc.scalar.activation(out=a0[:], in_=logit(n, eo, 0), func=ACT.Identity,
-                                     bias=bias(eo, 0), scale=1.0)
-                st[("a0", n, eo)] = a0
+        def bias(h, j):
+            return bcol[:, 2 * j + h % 2:2 * j + h % 2 + 1]
 
-        def maxima(n):
-            for eo in range(2):
-                st[("m", n, eo)] = soft.tile([P, 256], F32, name="m_%d" % eo)
-            for j in range(1, 4):
-                for eo in range(2):
-                    m = st[("m", n, eo)]
-                    prev = st[("a0", n, eo)] if j == 1 else m
-                    nc.vector.scalar_tensor_tensor(
-                        out=m[:], in0=logit(n, eo, j), scalar=bias(eo, j), in1=prev[:],
-                        op0=ALU.add, op1=ALU.max)
+        def first_gate(h):
+            a0 = soft.tile([P, 256], F32, name="a0")
+            nc.scalar.activation(out=a0[:], in_=logit(h, 0), func=ACT.Identity, bias=bias(h, 0), scale=1.0)
+            st[("m", h)] = a0
 
-        def shifts(n):
-            for eo in range(2):
-                e = soft.tile([P, 1024], F32, name="e_%d" % eo)
-                st[("e", n, eo)] = e
-                for j in range(4):
-                    nc.vector.scalar_tensor_tensor(
-                        out=e[:, j * 256:(j + 1) * 256], in0=logit(n, eo, j),
-                        scalar=bias(eo, j), in1=st[("m", n, eo)][:],
-                        op0=ALU.add, op1=ALU.subtract)
+        def maximum(h, j):
+            m = soft.tile([P, 256], F32, name="m%d" % j)
+            nc.vector.scalar_tensor_tensor(
+                out=m[:], in0=logit(h, j), scalar=bias(h, j), in1=st[("m", h)][:],
+                op0=ALU.add, op1=ALU.max)
+            st[("m", h)] = m
 
-        def exps(n):
-            for eo in range(2):
-                e = st[("e", n, eo)]
-                nc.scalar.activation(out=e[:], in_=e[:], func=ACT.Exp)
+        def shifts(h):
+            e = soft.tile([P, 1024], F32, name="e")
+            st[("e", h)] = e
+            for j in range(4):
+                nc.vector.scalar_tensor_tensor(
+                    out=e[:, j * 256:(j + 1) * 256], in0=logit(h, j),
+                    scalar=bias(h, j), in1=st[("m", h)][:],
+                    op0=ALU.add, op1=ALU.subtract)
 
-        def products(n, eo, eng):
-            gq, gb = st[("g", n)]
-            e = st[("e", n, eo)]
-            pr = soft.tile([P, 1024], F32, name="pr_%d" % eo)
-            st[("pr", n, eo)] = pr
-            for half, src in ((0, gq[:, 0:1024]), (1, gb[:])):
+        def exps(h):
+            e = st[("e", h)]
+            for g in range(2):
+                nc.scalar.activation(out=e[:, g * 512:(g + 1) * 512], in_=e[:, g * 512:(g + 1) * 512], func=ACT.Exp)
+
+        def products(h, eng):
+            n, eo = divmod(h, 2)
+            e = st[("e", h)]
+            pr = soft.tile([P, 1024], F32, name="pr")
+            st[("pr", h)] = pr
+            for half, src in ((0, st[("gq", n)][:, 0:1024]), (1, st[("gb", n)][:])):
                 sv = src.rearrange("p (c u e) -> p u e c", u=2, e=2)[:, :, eo, :]
                 eng.tensor_tensor(
                     out=pr[:, half * 512:(half + 1) * 512].rearrange("p (u c) -> p u c", u=2),
                     in0=e[:, half * 512:(half + 1) * 512].rearrange("p (u c) -> p u c", u=2),
                     in1=sv, op=ALU.mult)
 
-        def out_t(n):
-            den = ps.tile([P, 512], F32, name="den")
-            num = ps.tile([P, 512], F32, name="num")
-            st[("nd", n)] = (den, num)
-            for bank, key in ((den, "e"), (num, "pr")):
-                for eo in range(2):
-                    src = st[(key, n, eo)]
-                    for blk in range(2):
-                        c0 = blk * 256 + eo * 128
-                        for j in range(4):
-                            nc.tensor.matmul(
-                                out=bank[:, c0:c0 + 128],
-                                lhsT=src[:, j * 256 + blk * 128:j * 256 + blk * 128 + 128],
-                                rhs=ident[:], is_transpose=True,
-                                start=(j == 0), stop=(j == 3))
+        def sum_t(key, h):
+            n, eo = divmod(h, 2)
+            if eo == 0:
+                bank_new = ps.tile([P, 512], F32, name="bank_" + key)
+                st[("bank", key, n)] = bank_new
+            bank = st[("bank", key, n)]
+            src = st[(key, h)]
+            for blk in range(2):
+                c0 = blk * 256 + eo * 128
+                for j in range(4):
+                    nc.tensor.matmul(
+                        out=bank[:, c0:c0 + 128],
+                        lhsT=src[:, j * 256 + blk * 128:j * 256 + blk * 128 + 128],
+                        rhs=ident[:], is_transpose=True,
+                        start=(j == 0), stop=(j == 3))
 
         def bec(ap):
             return ap.rearrange("p (b e c) -> p b e c", b=2, e=2)
 
-        def swap_den(n):
-            den, num = st[("nd", n)]
-            dsw = fin.tile([P, 512], F32, name="dsw")
-            st[("dsw", n)] = dsw
-            for eo in range(2):
-                nc.scalar.copy(out=bec(dsw[:])[:, :, eo, :], in_=bec(den[:])[:, :, 1 - eo, :])
+        def swap_den(h):
+            n, eo = divmod(h, 2)
+            if eo == 0:
+                dsw_new = fin.tile([P, 512], F32, name="dsw")
+                st[("dsw", n)] = dsw_new
+            nc.scalar.copy(out=bec(st[("dsw", n)][:])[:, :, 1 - eo, :],
+                           in_=bec(st[("bank", "e", n)][:])[:, :, eo, :])
 
         def div_pp(n):
-            den, num = st[("nd", n)]
             pp = fin.tile([P, 256], F32, name="pp")
             st[("pp", n)] = pp
             nc.vector.tensor_tensor(out=pp[:].rearrange("p (b c) -> p b c", b=2),
-                                    in0=bec(den[:])[:, :, 0, :], in1=bec(st[("dsw", n)][:])[:, :, 0, :],
+                                    in0=bec(st[("bank", "e", n)][:])[:, :, 0, :],
+                                    in1=bec(st[("dsw", n)][:])[:, :, 0, :],
                                     op=ALU.mult)
 
         def div_cr(n):
-            den, num = st[("nd", n)]
             cr = fin.tile([P, 512], F32, name="cr")
             st[("cr", n)] = cr
-            nc.vector.tensor_tensor(out=cr[:], in0=num[:], in1=st[("dsw", n)][:], op=ALU.mult)
+            nc.vector.tensor_tensor(out=cr[:], in0=st[("bank", "pr", n)][:], in1=st[("dsw", n)][:], op=ALU.mult)
 
-        def div_r(n):
-            pp = st[("pp", n)]
-            rr = fin.tile([P, 256], F32, name="rr")
-            st[("rr", n)] = rr
-            nc.vector.reciprocal(out=rr[:], in_=pp[:])
+        def div_r(n, b):
+            if b == 0:
+                rr_new = fin.tile([P, 256], F32, name="rr")
+                st[("rr", n)] = rr_new
+            nc.vector.reciprocal(out=st[("rr", n)][:, b * 128:b * 128 + 128],
+                                 in_=st[("pp", n)][:, b * 128:b * 128 + 128])
 
         def div_out(n, eng):
-            cr = st[("cr", n)]
             osb = fin.tile([P, 512], F32, name="osb")
             eng.tensor_tensor(
                 out=osb[:].rearrange("p (b c e) -> p b c e", b=2, e=2),
-                in0=cr[:].rearrange("p (b e c) -> p b c e", b=2, e=2),
+                in0=st[("cr", n)][:].rearrange("p (b e c) -> p b c e", b=2, e=2),
                 in1=st[("rr", n)][:].rearrange("p (b c) -> p b c", b=2).unsqueeze(3).to_broadcast([P, 2, 128, 2]),
                 op=ALU.mult)
             nc.sync.dma_start(out=out_v[:, n, :], in_=osb[:])
@@ -278,61 +287,66 @@ def tile_multidimensinalgrucell_pb_t_kernel(
         def ok(n):
             return 0 <= n < N_PAIRS
 
-        in_t(0, 0)
-        evac(0, 0)
-        in_t(0, 1)
-        for j in range(4):
-            regroup_w(nc.vector.tensor_copy, 0, j)
-            regroup_w(nc.scalar.copy, 1, j)
-            if j == 0:
-                evac(0, 1)
-            else:
-                quant_w(j - 1)
-        quant(0)
-        quant_w(3)
+        in_q(0, 0)
+        evac_q(0, 0)
+        in_q(0, 1)
+        evac_q(0, 1)
+        regroup_w(nc.vector.tensor_copy, 0, 0)
+        regroup_w(nc.scalar.copy, 0, 1)
+        regroup_w(nc.vector.tensor_copy, 0, 2)
+        quant_w(0, 0)
+        quant(0, 0)
+        quant(0, 1)
+        regroup_w(nc.vector.tensor_copy, 0, 3)
+        quant_w(0, 1)
+        in_q(1, 0)
+        mx(0)
+        first_gate(0)
+        evac_q(1, 0)
+        in_q(1, 1)
+        evac_q(1, 1)
+        regroup_w(nc.vector.tensor_copy, 1, 0)
+        regroup_w(nc.scalar.copy, 1, 1)
+        regroup_w(nc.vector.tensor_copy, 1, 2)
+        quant_w(1, 0)
+        regroup_w(nc.vector.tensor_copy, 1, 3)
+        quant_w(1, 1)
+        in_b(0)
+        evac_b(0)
 
-        last = N_PAIRS - 1
-        for n in range(0, N_PAIRS + 1):
-            if ok(n + 4):
-                load(n + 4)
-            if n > 0 and ok(n + 1):
-                evac(n + 1, 1)
-                quant(n + 1)
-            if ok(n):
-                mx(n)
-                first_gate(n)
-            if n == 0:
-                in_t(1, 0)
-                evac(1, 0)
-                in_t(1, 1)
-                evac(1, 1)
+        for h in range(HALVES + 4):
+            n, eo = divmod(h, 2)
+            if eo == 0 and ok(n + 5):
+                load(n + 5)
+            if h + 1 < HALVES:
+                mx(h + 1)
+            if 1 <= h <= HALVES:
+                exps(h - 1)
+                products(h - 1, nc.gpsimd)
+            if eo == 0:
+                fill = [(ok(n - 2), lambda: div_cr(n - 2)), (ok(n + 1), lambda: quant(n + 1, 0)), (ok(n + 1), lambda: quant(n + 1, 1))]
+            else:
+                fill = [(ok(n - 1), lambda: div_pp(n - 1)), (ok(n - 1), lambda: div_r(n - 1, 0)), (ok(n - 1), lambda: div_r(n - 1, 1))]
+            for i in range(3):
+                if h < HALVES:
+                    maximum(h, i + 1)
+                if fill[i][0]:
+                    fill[i][1]()
+            if h < HALVES:
+                shifts(h)
+            if eo == 0 and ok(n - 2):
+                div_out(n - 2, nc.gpsimd)
+            if h + 1 < HALVES:
+                first_gate(h + 1)
             if ok(n + 2):
-                in_t(n + 2, 0)
-                evac(n + 2, 0)
-            if ok(n):
-                maxima(n)
-                shifts(n)
-            if n == 0:
-                quant(1)
-            if ok(n - 1):
-                out_t(n - 1)
-                swap_den(n - 1)
-            if ok(n):
-                exps(n)
-                products(n, 0, nc.gpsimd)
-                if n < last:
-                    products(n, 1, nc.gpsimd)
-            if ok(n + 2):
-                in_t(n + 2, 1)
-            if ok(n - 1) and n - 1 < last:
-                div_pp(n - 1)
-                div_cr(n - 1)
-                div_r(n - 1)
-                div_out(n - 1, nc.gpsimd)
-            if n == last:
-                products(n, 1, nc.vector)
-            if n - 1 == last:
-                div_pp(last)
-                div_r(last)
-                div_cr(last)
-                div_out(last, nc.vector)
+                in_q(n + 2, eo)
+                evac_q(n + 2, eo)
+            if 1 <= h <= HALVES:
+                sum_t("e", h - 1)
+            if eo == 1 and ok(n + 1):
+                in_b(n + 1)
+                evac_b(n + 1)
+            if 1 <= h <= HALVES:
+                swap_den(h - 1)
+            if 2 <= h <= HALVES + 1:
+                sum_t("pr", h - 2)

@@ -15,6 +15,7 @@ P = 128
 BATCH = 4096
 UNITS = 256
 N_PAIRS = 16
+LOG_GROUPS = ((0, 4), (4, 4), (8, 3))
 HALVES = 2 * N_PAIRS
 FLOPS = 2 * BATCH * 1024 * 1024
 
@@ -42,6 +43,9 @@ def tile_multidimensinalgrucell_pb_t_kernel(
         grp = ctx.enter_context(tc.tile_pool(name="grp", bufs=5))
         qnt = ctx.enter_context(tc.tile_pool(name="qnt", bufs=2))
         soft = ctx.enter_context(tc.tile_pool(name="soft", bufs=3))
+        deep = ctx.enter_context(tc.tile_pool(name="deep", bufs=6))
+        grpd = ctx.enter_context(tc.tile_pool(name="grpd", bufs=2))
+        late = ctx.enter_context(tc.tile_pool(name="late", bufs=8))
         fin = ctx.enter_context(tc.tile_pool(name="fin", bufs=3))
         ps = ctx.enter_context(tc.psum_pool(name="ps", bufs=1))
         ps2 = ctx.enter_context(tc.psum_pool(name="ps2", bufs=2))
@@ -152,16 +156,11 @@ def tile_multidimensinalgrucell_pb_t_kernel(
                 in_=st[("tb", n)][:].rearrange("p (s c) -> p c s", s=2),
             )
 
-        def quant(n, s):
-            if s == 0:
-                qc_new = qnt.tile([P, 512], U32, name="qc", align_bytes=64)
-                qs_new = qnt.tile([P, 512], U8, name="qs", align_bytes=64)
-                st[("q", n)] = (qc_new, qs_new)
-            qc, qs = st[("q", n)]
-            nc.vector.quantize_mx(
-                out=qc[:, s * 256:(s + 1) * 256].bitcast(FP8X4),
-                scales=qs[:, s * 256:(s + 1) * 256],
-                in_=st[("gq", n)][:, s * 1024:(s + 1) * 1024])
+        def quant(n):
+            qc = qnt.tile([P, 512], U32, name="qc", align_bytes=64)
+            qs = qnt.tile([P, 512], U8, name="qs", align_bytes=64)
+            nc.vector.quantize_mx(out=qc[:].bitcast(FP8X4), scales=qs[:], in_=st[("gq", n)][:])
+            st[("q", n)] = (qc, qs)
 
         def mx(h):
             n, eo = divmod(h, 2)
@@ -203,7 +202,7 @@ def tile_multidimensinalgrucell_pb_t_kernel(
             st[("m", h)] = m
 
         def shifts(h):
-            e = soft.tile([P, 1024], F32, name="e")
+            e = deep.tile([P, 1024], F32, name="e")
             st[("e", h)] = e
             for j in range(4):
                 nc.vector.scalar_tensor_tensor(
@@ -219,7 +218,7 @@ def tile_multidimensinalgrucell_pb_t_kernel(
         def products(h, eng):
             n, eo = divmod(h, 2)
             e = st[("e", h)]
-            pr = soft.tile([P, 1024], F32, name="pr")
+            pr = deep.tile([P, 1024], F32, name="pr")
             st[("pr", h)] = pr
             for half, src in ((0, st[("gq", n)][:, 0:1024]), (1, st[("gb", n)][:])):
                 sv = src.rearrange("p (c u e) -> p u e c", u=2, e=2)[:, :, eo, :]
@@ -252,35 +251,56 @@ def tile_multidimensinalgrucell_pb_t_kernel(
             if eo == 0:
                 dsw_new = fin.tile([P, 512], F32, name="dsw")
                 st[("dsw", n)] = dsw_new
-            nc.scalar.copy(out=bec(st[("dsw", n)][:])[:, :, 1 - eo, :],
-                           in_=bec(st[("bank", "e", n)][:])[:, :, eo, :])
+            nc.vector.tensor_copy(out=bec(st[("dsw", n)][:])[:, :, 1 - eo, :],
+                                  in_=bec(st[("bank", "e", n)][:])[:, :, eo, :])
 
         def div_pp(n):
-            pp = fin.tile([P, 256], F32, name="pp")
-            st[("pp", n)] = pp
-            nc.vector.tensor_tensor(out=pp[:].rearrange("p (b c) -> p b c", b=2),
+            first, size = group_of(n)
+            if size == 1:
+                pp_one = fin.tile([P, 256], F32, name="pp_one")
+                rr_one = fin.tile([P, 256], F32, name="rr_one")
+                st[("pp", n)], st[("rr", n)] = pp_one, rr_one
+            elif n == first:
+                pp_new = grpd.tile([P, 1024], F32, name="pp")
+                rr_new = grpd.tile([P, 1024], F32, name="rr")
+                st[("pp", first)], st[("rr", first)] = pp_new, rr_new
+            c0 = (n - first) * 256
+            nc.vector.tensor_tensor(out=st[("pp", first)][:, c0:c0 + 256].rearrange("p (b c) -> p b c", b=2),
                                     in0=bec(st[("bank", "e", n)][:])[:, :, 0, :],
                                     in1=bec(st[("dsw", n)][:])[:, :, 0, :],
                                     op=ALU.mult)
 
+        def group_of(n):
+            for first, size in LOG_GROUPS:
+                if first <= n < first + size:
+                    return first, size
+            return n, 1
+
+        def group_ln(first, size):
+            pp = st[("pp", first)]
+            nc.scalar.activation(out=pp[:, 0:size * 256], in_=pp[:, 0:size * 256], func=ACT.Ln)
+
+        def group_exp(first, size):
+            nc.scalar.activation(out=st[("rr", first)][:, 0:size * 256], in_=st[("pp", first)][:, 0:size * 256],
+                                 func=ACT.Exp, scale=-1.0)
+
         def div_cr(n):
-            cr = fin.tile([P, 512], F32, name="cr")
+            cr = late.tile([P, 512], F32, name="cr")
             st[("cr", n)] = cr
             nc.vector.tensor_tensor(out=cr[:], in0=st[("bank", "pr", n)][:], in1=st[("dsw", n)][:], op=ALU.mult)
 
         def div_r(n, b):
-            if b == 0:
-                rr_new = fin.tile([P, 256], F32, name="rr")
-                st[("rr", n)] = rr_new
             nc.vector.reciprocal(out=st[("rr", n)][:, b * 128:b * 128 + 128],
                                  in_=st[("pp", n)][:, b * 128:b * 128 + 128])
 
         def div_out(n, eng):
+            first, size = group_of(n)
+            r0 = (n - first) * 256
             osb = fin.tile([P, 512], F32, name="osb")
             eng.tensor_tensor(
                 out=osb[:].rearrange("p (b c e) -> p b c e", b=2, e=2),
                 in0=st[("cr", n)][:].rearrange("p (b e c) -> p b c e", b=2, e=2),
-                in1=st[("rr", n)][:].rearrange("p (b c) -> p b c", b=2).unsqueeze(3).to_broadcast([P, 2, 128, 2]),
+                in1=st[("rr", first)][:, r0:r0 + 256].rearrange("p (b c) -> p b c", b=2).unsqueeze(3).to_broadcast([P, 2, 128, 2]),
                 op=ALU.mult)
             nc.sync.dma_start(out=out_v[:, n, :], in_=osb[:])
 
@@ -295,8 +315,7 @@ def tile_multidimensinalgrucell_pb_t_kernel(
         regroup_w(nc.scalar.copy, 0, 1)
         regroup_w(nc.vector.tensor_copy, 0, 2)
         quant_w(0, 0)
-        quant(0, 0)
-        quant(0, 1)
+        quant(0)
         regroup_w(nc.vector.tensor_copy, 0, 3)
         quant_w(0, 1)
         in_q(1, 0)
@@ -314,39 +333,59 @@ def tile_multidimensinalgrucell_pb_t_kernel(
         in_b(0)
         evac_b(0)
 
-        for h in range(HALVES + 4):
+        ln_slot, exp_slot = {}, {}
+        out_slot = {h: [] for h in range(HALVES + 8)}
+        for first, size in LOG_GROUPS:
+            s = 2 * (first + size - 1) + 6
+            ln_slot[s] = (first, size)
+            exp_slot[s + 4] = (first, size)
+            for i in range(size):
+                out_slot[s + 5 + i].append(first + i)
+        for n in range(N_PAIRS):
+            if group_of(n)[1] == 1:
+                out_slot[2 * n + 7].append(n)
+        for h in range(HALVES + 8):
             n, eo = divmod(h, 2)
             if eo == 0 and ok(n + 5):
                 load(n + 5)
             if h + 1 < HALVES:
                 mx(h + 1)
+            after_ln = any(0 < h - s <= 3 for s in ln_slot)
+            if after_ln and h + 1 < HALVES:
+                first_gate(h + 1)
             if 1 <= h <= HALVES:
                 exps(h - 1)
-                products(h - 1, nc.gpsimd)
+                products(h - 1, nc.gpsimd if h < HALVES else nc.vector)
+            q = n - 2
             if eo == 0:
-                fill = [(ok(n - 2), lambda: div_cr(n - 2)), (ok(n + 1), lambda: quant(n + 1, 0)), (ok(n + 1), lambda: quant(n + 1, 1))]
+                fill = [(ok(n - 3), lambda: div_cr(n - 3)), (ok(n + 1), lambda: quant(n + 1)), (ok(q), lambda: swap_den(2 * q))]
             else:
-                fill = [(ok(n - 1), lambda: div_pp(n - 1)), (ok(n - 1), lambda: div_r(n - 1, 0)), (ok(n - 1), lambda: div_r(n - 1, 1))]
+                fill = [(ok(q), lambda: swap_den(2 * q + 1)), (ok(q), lambda: div_pp(q)), (False, None)]
             for i in range(3):
                 if h < HALVES:
                     maximum(h, i + 1)
                 if fill[i][0]:
                     fill[i][1]()
+            if eo == 0 and ok(n - 3) and group_of(n - 3)[1] == 1:
+                div_r(n - 3, 0)
+                div_r(n - 3, 1)
             if h < HALVES:
                 shifts(h)
-            if eo == 0 and ok(n - 2):
-                div_out(n - 2, nc.gpsimd)
-            if h + 1 < HALVES:
+            for m in out_slot[h]:
+                div_out(m, nc.gpsimd if h < HALVES + 2 else nc.vector)
+            if not after_ln and h + 1 < HALVES:
                 first_gate(h + 1)
             if ok(n + 2):
                 in_q(n + 2, eo)
                 evac_q(n + 2, eo)
-            if 1 <= h <= HALVES:
-                sum_t("e", h - 1)
             if eo == 1 and ok(n + 1):
                 in_b(n + 1)
                 evac_b(n + 1)
-            if 1 <= h <= HALVES:
-                swap_den(h - 1)
-            if 2 <= h <= HALVES + 1:
-                sum_t("pr", h - 2)
+            if h in ln_slot:
+                group_ln(*ln_slot[h])
+            if h in exp_slot:
+                group_exp(*exp_slot[h])
+            if 0 <= h - 4 < HALVES:
+                sum_t("pr", h - 4)
+            if 0 <= h - 3 < HALVES:
+                sum_t("e", h - 3)

@@ -15,7 +15,8 @@ P = 128
 BATCH = 4096
 UNITS = 256
 N_PAIRS = 16
-LOG_GROUPS = ((0, 4), (4, 4), (8, 3))
+LOG_GROUPS = ((0, 4), (4, 4), (8, 4), (12, 2))
+LD = 3
 HALVES = 2 * N_PAIRS
 FLOPS = 2 * BATCH * 1024 * 1024
 
@@ -32,10 +33,10 @@ def tile_multidimensinalgrucell_pb_t_kernel(
         return a.rearrange("(p n t) f -> p n (t f)", n=N_PAIRS, t=2)
 
     def rows3(a):
-        return a.rearrange("(p n t) f -> p n t f", n=N_PAIRS, t=2)
+        return a.rearrange("(p n t) (a f) -> p n (t a) f", n=N_PAIRS, t=2, a=2)
 
     left_v, top_v, h_v, out_v = rows(left_state), rows(top_state), rows(h_cand), rows(out)
-    diag_v, x_v = rows3(diagonal_state), rows3(x)
+    diag_v, x_v, dg_v = rows3(diagonal_state), rows3(x), rows(diagonal_state)
 
     with ExitStack() as ctx:
         const = ctx.enter_context(tc.tile_pool(name="const", bufs=1))
@@ -57,14 +58,16 @@ def tile_multidimensinalgrucell_pb_t_kernel(
             lf = inp.tile([P, 512], BF16, name="lf")
             tp = inp.tile([P, 512], BF16, name="tp")
             dx = inp.tile([P, 1024], BF16, name="dx")
+            dg = inp.tile([P, 512], BF16, name="dg")
             hc = inp.tile([P, 512], BF16, name="hc")
-            dx4 = dx[:].rearrange("p (t s f) -> p t s f", t=2, s=2)
+            dx4 = dx[:].rearrange("p (y s f) -> p y s f", y=4, s=2)
             nc.sync.dma_start(out=lf[:], in_=left_v[:, n, :])
             nc.sync.dma_start(out=tp[:], in_=top_v[:, n, :])
             nc.sync.dma_start(out=dx4[:, :, 0, :], in_=diag_v[:, n])
             nc.sync.dma_start(out=dx4[:, :, 1, :], in_=x_v[:, n])
             nc.sync.dma_start(out=hc[:], in_=h_v[:, n, :])
-            st[("in", n)] = (lf, tp, dx, hc)
+            nc.sync.dma_start(out=dg[:], in_=dg_v[:, n, :])
+            st[("in", n)] = (lf, tp, dx, hc, dg)
 
         ident = const.tile([P, P], F32, name="ident")
         make_identity(nc, ident[:])
@@ -82,10 +85,11 @@ def tile_multidimensinalgrucell_pb_t_kernel(
                 out=wraw[:, j * 2048:j * 2048 + 1024].rearrange("p (u y) -> p u y", u=2),
                 in_=gate_w[j][0:512, :].rearrange("(u p e) c -> p u (e c)", u=2, e=2),
             )
-            nc.sync.dma_start(
-                out=wraw[:, j * 2048 + 1024:(j + 1) * 2048],
-                in_=gate_w[j][512:1024, :].rearrange("(p t) c -> p (t c)", t=4),
-            )
+            for g in range(2):
+                nc.sync.dma_start(
+                    out=wraw[g * 64:(g + 1) * 64, j * 2048 + 1024:(j + 1) * 2048].rearrange("p (u y) -> p u y", u=2),
+                    in_=gate_w[j][512 + g * 256:768 + g * 256, :].rearrange("(u p e) c -> p u (e c)", u=2, e=2),
+                )
         load(1)
         load(2)
         load(3)
@@ -116,16 +120,19 @@ def tile_multidimensinalgrucell_pb_t_kernel(
                 in_=wg[:, g0 * 1024:(g0 + 2) * 1024],
             )
 
+        def gp_copy(out, in_):
+            nc.gpsimd.tensor_scalar(out=out, in0=in_, scalar1=1.0, scalar2=0.0, op0=ALU.mult, op1=ALU.add)
+
         def in_q(n, tl):
-            lf, tp, dx, hc = st[("in", n)]
+            lf, tp, dx, hc, dg = st[("in", n)]
             tr = ps2.tile([P, 512], F32, name="tr")
             lfw, tpw, dxw = [a[:].bitcast(F32) for a in (lf, tp, dx)]
             w0 = tl * 128
             d0 = tl * 256
             nc.tensor.transpose(tr[:, 0:128], lfw[:, w0:w0 + 128], ident[:])
             nc.tensor.transpose(tr[:, 128:256], tpw[:, w0:w0 + 128], ident[:])
-            nc.tensor.transpose(tr[:, 256:384], dxw[:, d0:d0 + 256:2], ident[:])
-            nc.tensor.transpose(tr[:, 384:512], dxw[:, d0 + 1:d0 + 256:2], ident[:])
+            nc.tensor.transpose(tr[:, 256:384], dxw[:, d0:d0 + 128], ident[:])
+            nc.tensor.transpose(tr[:, 384:512], dxw[:, d0 + 128:d0 + 256], ident[:])
             st[("tr", n, tl)] = tr
 
         def evac_q(n, tl):
@@ -139,11 +146,11 @@ def tile_multidimensinalgrucell_pb_t_kernel(
             )
 
         def in_b(n):
-            lf, tp, dx, hc = st[("in", n)]
+            lf, tp, dx, hc, dg = st[("in", n)]
             tb = ps2.tile([P, 512], F32, name="tr")
-            dxw, hcw = [a[:].bitcast(F32) for a in (dx, hc)]
+            dgw, hcw = [a[:].bitcast(F32) for a in (dg, hc)]
             for tl in range(2):
-                nc.tensor.transpose(tb[:, tl * 128:tl * 128 + 128], dxw[:, tl * 256:tl * 256 + 128], ident[:])
+                nc.tensor.transpose(tb[:, tl * 128:tl * 128 + 128], dgw[:, tl * 128:tl * 128 + 128], ident[:])
             for tl in range(2):
                 nc.tensor.transpose(tb[:, 256 + tl * 128:384 + tl * 128], hcw[:, tl * 128:tl * 128 + 128], ident[:])
             st[("tb", n)] = tb
@@ -162,14 +169,12 @@ def tile_multidimensinalgrucell_pb_t_kernel(
             nc.vector.quantize_mx(out=qc[:].bitcast(FP8X4), scales=qs[:], in_=st[("gq", n)][:])
             st[("q", n)] = (qc, qs)
 
-        def mx(h):
+        def mx(h, g):
             n, eo = divmod(h, 2)
             qc, qs = st[("q", n)]
-            la = ps.tile([P, 512], F32, name="la%d" % eo)
-            lb = ps.tile([P, 512], F32, name="lb%d" % eo)
-            st[("l", h)] = (la, lb)
-            for j in range(4):
-                bank = (la, lb)[j // 2]
+            bank = ps.tile([P, 512], F32, name="l%d%d" % (g, eo))
+            st[("l", h, g)] = bank
+            for j in range(2 * g, 2 * g + 2):
                 c0 = (j % 2) * 256
                 for s in range(2):
                     b0 = ((eo * 4 + j) * 2 + s) * 128
@@ -184,7 +189,7 @@ def tile_multidimensinalgrucell_pb_t_kernel(
                     )
 
         def logit(h, j):
-            return st[("l", h)][j // 2][:, (j % 2) * 256:(j % 2) * 256 + 256]
+            return st[("l", h, j // 2)][:, (j % 2) * 256:(j % 2) * 256 + 256]
 
         def bias(h, j):
             return bcol[:, 2 * j + h % 2:2 * j + h % 2 + 1]
@@ -296,7 +301,7 @@ def tile_multidimensinalgrucell_pb_t_kernel(
         def div_out(n, eng):
             first, size = group_of(n)
             r0 = (n - first) * 256
-            osb = fin.tile([P, 512], F32, name="osb")
+            osb = late.tile([P, 512], F32, name="osb")
             eng.tensor_tensor(
                 out=osb[:].rearrange("p (b c e) -> p b c e", b=2, e=2),
                 in0=st[("cr", n)][:].rearrange("p (b e c) -> p b c e", b=2, e=2),
@@ -312,80 +317,109 @@ def tile_multidimensinalgrucell_pb_t_kernel(
         in_q(0, 1)
         evac_q(0, 1)
         regroup_w(nc.vector.tensor_copy, 0, 0)
-        regroup_w(nc.scalar.copy, 0, 1)
-        regroup_w(nc.vector.tensor_copy, 0, 2)
-        quant_w(0, 0)
+        regroup_w(nc.vector.tensor_copy, 0, 1)
         quant(0)
-        regroup_w(nc.vector.tensor_copy, 0, 3)
-        quant_w(0, 1)
+        quant_w(0, 0)
+        regroup_w(nc.scalar.copy, 1, 0)
+        regroup_w(nc.scalar.copy, 1, 1)
         in_q(1, 0)
-        mx(0)
+        mx(0, 0)
         first_gate(0)
         evac_q(1, 0)
+        regroup_w(nc.vector.tensor_copy, 0, 2)
+        regroup_w(nc.vector.tensor_copy, 0, 3)
+        quant_w(0, 1)
         in_q(1, 1)
+        mx(0, 1)
         evac_q(1, 1)
-        regroup_w(nc.vector.tensor_copy, 1, 0)
-        regroup_w(nc.scalar.copy, 1, 1)
-        regroup_w(nc.vector.tensor_copy, 1, 2)
-        quant_w(1, 0)
-        regroup_w(nc.vector.tensor_copy, 1, 3)
-        quant_w(1, 1)
+        regroup_w(nc.scalar.copy, 1, 2)
+        regroup_w(gp_copy, 1, 3)
+        in_q(2, 0)
+        evac_q(2, 0)
         in_b(0)
         evac_b(0)
 
-        ln_slot, exp_slot = {}, {}
-        out_slot = {h: [] for h in range(HALVES + 8)}
+        def den_slot(k):
+            return min(k + LD, max(k + 1, k // 2 + N_PAIRS))
+
+        def num_slot(k):
+            return min(k + LD + 1, max(k + 2, k // 2 + N_PAIRS + 1))
+
+        END = HALVES + 4
+        ln_at, exp_at = {}, {}
+        outs = {h: [] for h in range(END + 20)}
         for first, size in LOG_GROUPS:
-            s = 2 * (first + size - 1) + 6
-            ln_slot[s] = (first, size)
-            exp_slot[s + 4] = (first, size)
+            s = den_slot(2 * (first + size) - 1) + 2
+            ln_at[s] = (first, size)
+            exp_at[min(s + 3, HALVES)] = (first, size)
             for i in range(size):
-                out_slot[s + 5 + i].append(first + i)
-        for n in range(N_PAIRS):
-            if group_of(n)[1] == 1:
-                out_slot[2 * n + 7].append(n)
-        for h in range(HALVES + 8):
+                outs[min(s + 4 + i, HALVES + 1)].append(first + i)
+        last = N_PAIRS - 1
+        outs[END - 2] += [last - 1, last]
+        for h in range(END):
             n, eo = divmod(h, 2)
             if eo == 0 and ok(n + 5):
                 load(n + 5)
-            if h + 1 < HALVES:
-                mx(h + 1)
-            after_ln = any(0 < h - s <= 3 for s in ln_slot)
-            if after_ln and h + 1 < HALVES:
-                first_gate(h + 1)
+            if 0 < h < HALVES - 1:
+                mx(h + 1, 0)
+            after_ln = any(0 < h - s <= 3 for s in ln_at)
+            nq, tq = divmod(h + 5, 2)
+            if ok(nq):
+                in_q(nq, tq)
+            if after_ln:
+                if h + 1 < HALVES:
+                    first_gate(h + 1)
+                if ok(nq):
+                    evac_q(nq, tq)
             if 1 <= h <= HALVES:
                 exps(h - 1)
-                products(h - 1, nc.gpsimd if h < HALVES else nc.vector)
-            q = n - 2
-            if eo == 0:
-                fill = [(ok(n - 3), lambda: div_cr(n - 3)), (ok(n + 1), lambda: quant(n + 1)), (ok(q), lambda: swap_den(2 * q))]
-            else:
-                fill = [(ok(q), lambda: swap_den(2 * q + 1)), (ok(q), lambda: div_pp(q)), (False, None)]
-            for i in range(3):
+                products(h - 1, nc.gpsimd)
+            fill = []
+            for q in range(N_PAIRS):
+                if num_slot(2 * q + 1) + 1 == h:
+                    fill.append((div_cr, q))
+            for k in range(HALVES):
+                if den_slot(k) + 1 == h:
+                    fill.append((swap_den, k))
+                    if k % 2:
+                        fill.append((div_pp, k // 2))
+                        if k // 2 >= last - 1:
+                            fill.append((lambda q: (div_r(q, 0), div_r(q, 1)), k // 2))
+            if h == 0:
+                fill = [(lambda q: quant_w(1, 0), 0), (lambda q: quant_w(1, 1), 0), (quant, 1)]
+            elif eo == 0 and ok(n + 1):
+                quant(n + 1)
+            for j in range(1, 4):
                 if h < HALVES:
-                    maximum(h, i + 1)
-                if fill[i][0]:
-                    fill[i][1]()
-            if eo == 0 and ok(n - 3) and group_of(n - 3)[1] == 1:
-                div_r(n - 3, 0)
-                div_r(n - 3, 1)
+                    maximum(h, j)
+                if fill:
+                    f, arg = fill.pop(0)
+                    f(arg)
             if h < HALVES:
                 shifts(h)
-            for m in out_slot[h]:
-                div_out(m, nc.gpsimd if h < HALVES + 2 else nc.vector)
-            if not after_ln and h + 1 < HALVES:
-                first_gate(h + 1)
-            if ok(n + 2):
-                in_q(n + 2, eo)
-                evac_q(n + 2, eo)
+            if h == 0:
+                mx(1, 0)
+            for f, arg in fill:
+                f(arg)
+            for m in outs[h]:
+                div_out(m, nc.vector if m == last else nc.gpsimd)
+            for k in range(HALVES):
+                if num_slot(k) == h:
+                    sum_t("pr", k)
+            if not after_ln:
+                if h + 1 < HALVES:
+                    first_gate(h + 1)
+                if ok(nq):
+                    evac_q(nq, tq)
+            if h + 1 < HALVES:
+                mx(h + 1, 1)
             if eo == 1 and ok(n + 1):
                 in_b(n + 1)
                 evac_b(n + 1)
-            if h in ln_slot:
-                group_ln(*ln_slot[h])
-            if h in exp_slot:
-                group_exp(*exp_slot[h])
-            if 0 <= h - 4 < HALVES:
-                sum_t("pr", h - 4)
-            if 0 <= h - 3 < HALVES:
-                sum_t("e", h - 3)
+            if h in ln_at:
+                group_ln(*ln_at[h])
+            if h in exp_at:
+                group_exp(*exp_at[h])
+            for k in range(HALVES):
+                if den_slot(k) == h:
+                    sum_t("e", k)

@@ -12,10 +12,11 @@ ACT = mybir.ActivationFunctionType
 ALU = mybir.AluOpType
 
 P = 128
+KEEP = 128
 BATCH = 4096
 UNITS = 256
 N_PAIRS = 16
-LOG_GROUPS = ((0, 4), (4, 4), (8, 4), (12, 2))
+LOG_GROUPS = ((0, 4), (4, 4), (8, 4), (12, 3))
 LD = 3
 HALVES = 2 * N_PAIRS
 FLOPS = 2 * BATCH * 1024 * 1024
@@ -46,6 +47,7 @@ def tile_multidimensinalgrucell_pb_t_kernel(
         soft = ctx.enter_context(tc.tile_pool(name="soft", bufs=3))
         deep = ctx.enter_context(tc.tile_pool(name="deep", bufs=6))
         grpd = ctx.enter_context(tc.tile_pool(name="grpd", bufs=2))
+        stor = ctx.enter_context(tc.tile_pool(name="stor", bufs=4))
         late = ctx.enter_context(tc.tile_pool(name="late", bufs=8))
         fin = ctx.enter_context(tc.tile_pool(name="fin", bufs=3))
         ps = ctx.enter_context(tc.psum_pool(name="ps", bufs=1))
@@ -71,6 +73,8 @@ def tile_multidimensinalgrucell_pb_t_kernel(
 
         ident = const.tile([P, P], F32, name="ident")
         make_identity(nc, ident[:])
+        spare = const.tile([P, 256], BF16, name="spare")
+        nc.gpsimd.memset(spare[:], 0.0)
         brow = const.tile([P, 256], BF16, name="brow")
         nc.vector.memset(brow[:], 0.0)
         warm = const.tile([P, 8], F32, name="warm")
@@ -174,6 +178,7 @@ def tile_multidimensinalgrucell_pb_t_kernel(
             qc, qs = st[("q", n)]
             bank = ps.tile([P, 512], F32, name="l%d%d" % (g, eo))
             st[("l", h, g)] = bank
+            nc.tensor.matmul(out=bank[:, 0:KEEP], lhsT=spare[:, 0:128], rhs=spare[:, 0:KEEP], start=True, stop=True)
             for j in range(2 * g, 2 * g + 2):
                 c0 = (j % 2) * 256
                 for s in range(2):
@@ -285,8 +290,9 @@ def tile_multidimensinalgrucell_pb_t_kernel(
             pp = st[("pp", first)]
             nc.scalar.activation(out=pp[:, 0:size * 256], in_=pp[:, 0:size * 256], func=ACT.Ln)
 
-        def group_exp(first, size):
-            nc.scalar.activation(out=st[("rr", first)][:, 0:size * 256], in_=st[("pp", first)][:, 0:size * 256],
+        def group_exp(first, size, skip=0):
+            a, b = skip * 256, (skip + size) * 256
+            nc.scalar.activation(out=st[("rr", first)][:, a:b], in_=st[("pp", first)][:, a:b],
                                  func=ACT.Exp, scale=-1.0)
 
         def div_cr(n):
@@ -301,7 +307,7 @@ def tile_multidimensinalgrucell_pb_t_kernel(
         def div_out(n, eng):
             first, size = group_of(n)
             r0 = (n - first) * 256
-            osb = late.tile([P, 512], F32, name="osb")
+            osb = stor.tile([P, 512], F32, name="osb")
             eng.tensor_tensor(
                 out=osb[:].rearrange("p (b c e) -> p b c e", b=2, e=2),
                 in0=st[("cr", n)][:].rearrange("p (b e c) -> p b c e", b=2, e=2),
@@ -350,12 +356,18 @@ def tile_multidimensinalgrucell_pb_t_kernel(
         outs = {h: [] for h in range(END + 20)}
         for first, size in LOG_GROUPS:
             s = den_slot(2 * (first + size) - 1) + 2
+            if first + size == N_PAIRS - 1:
+                ln_at[HALVES] = (first, size)
+                exp_at[HALVES] = (first, size)
+                outs[END - 1] += list(range(first, first + size))
+                continue
             ln_at[s] = (first, size)
-            exp_at[min(s + 3, HALVES)] = (first, size)
+            exp_at[s + 3] = (first, size)
             for i in range(size):
-                outs[min(s + 4 + i, HALVES + 1)].append(first + i)
+                o = s + 4 + i
+                outs[o if o < HALVES - 3 else HALVES + 1].append(first + i)
         last = N_PAIRS - 1
-        outs[END - 2] += [last - 1, last]
+        outs[END - 2].append(last)
         for h in range(END):
             n, eo = divmod(h, 2)
             if eo == 0 and ok(n + 5):
@@ -383,7 +395,7 @@ def tile_multidimensinalgrucell_pb_t_kernel(
                     fill.append((swap_den, k))
                     if k % 2:
                         fill.append((div_pp, k // 2))
-                        if k // 2 >= last - 1:
+                        if k // 2 == last:
                             fill.append((lambda q: (div_r(q, 0), div_r(q, 1)), k // 2))
             if h == 0:
                 fill = [(lambda q: quant_w(1, 0), 0), (lambda q: quant_w(1, 1), 0), (quant, 1)]
@@ -402,7 +414,11 @@ def tile_multidimensinalgrucell_pb_t_kernel(
             for f, arg in fill:
                 f(arg)
             for m in outs[h]:
-                div_out(m, nc.vector if m == last else nc.gpsimd)
+                div_out(m, nc.vector if h >= HALVES else nc.gpsimd)
+            if h >= HALVES:
+                for k in range(HALVES):
+                    if den_slot(k) == h:
+                        sum_t("e", k)
             for k in range(HALVES):
                 if num_slot(k) == h:
                     sum_t("pr", k)
@@ -419,7 +435,12 @@ def tile_multidimensinalgrucell_pb_t_kernel(
             if h in ln_at:
                 group_ln(*ln_at[h])
             if h in exp_at:
-                group_exp(*exp_at[h])
-            for k in range(HALVES):
-                if den_slot(k) == h:
-                    sum_t("e", k)
+                if h < HALVES:
+                    group_exp(*exp_at[h])
+                else:
+                    for m in range(exp_at[h][1]):
+                        group_exp(exp_at[h][0], 1, m)
+            if h < HALVES:
+                for k in range(HALVES):
+                    if den_slot(k) == h:
+                        sum_t("e", k)

@@ -211,19 +211,21 @@ def tile_multidimensinalgrucell_pb_t_kernel(
                 op0=ALU.add, op1=ALU.max)
             st[("m", h)] = m
 
-        def shifts(h):
-            e = deep.tile([P, 1024], F32, name="e")
-            st[("e", h)] = e
-            for j in range(4):
-                nc.vector.scalar_tensor_tensor(
-                    out=e[:, j * 256:(j + 1) * 256], in0=logit(h, j),
-                    scalar=bias(h, j), in1=st[("m", h)][:],
-                    op0=ALU.add, op1=ALU.subtract)
+        def shift(h, g):
+            if g == 0:
+                e_new = deep.tile([P, 1024], F32, name="e")
+                st[("e", h)] = e_new
+            nc.vector.tensor_tensor(
+                out=st[("e", h)][:, g * 512:(g + 1) * 512].rearrange("p (j c) -> p j c", j=2),
+                in0=st[("l", h, g)][:].rearrange("p (j c) -> p j c", j=2),
+                in1=st[("m", h)][:].unsqueeze(1).to_broadcast([P, 2, 256]),
+                op=ALU.subtract)
 
-        def exps(h):
+        def exps(h, g):
             e = st[("e", h)]
-            for g in range(2):
-                nc.scalar.activation(out=e[:, g * 512:(g + 1) * 512], in_=e[:, g * 512:(g + 1) * 512], func=ACT.Exp)
+            for j in range(2 * g, 2 * g + 2):
+                nc.scalar.activation(out=e[:, j * 256:(j + 1) * 256], in_=e[:, j * 256:(j + 1) * 256],
+                                     func=ACT.Exp, bias=bias(h, j), scale=1.0)
 
         def products(h, eng):
             n, eo = divmod(h, 2)
@@ -245,7 +247,7 @@ def tile_multidimensinalgrucell_pb_t_kernel(
             bank = st[("bank", key, n)]
             src = st[(key, h)]
             for blk in range(2):
-                c0 = blk * 256 + eo * 128
+                c0 = blk * 256 + (1 - eo if key == "e" else eo) * 128
                 for j in range(4):
                     nc.tensor.matmul(
                         out=bank[:, c0:c0 + 128],
@@ -256,13 +258,10 @@ def tile_multidimensinalgrucell_pb_t_kernel(
         def bec(ap):
             return ap.rearrange("p (b e c) -> p b e c", b=2, e=2)
 
-        def swap_den(h):
-            n, eo = divmod(h, 2)
-            if eo == 0:
-                dsw_new = fin.tile([P, 512], F32, name="dsw")
-                st[("dsw", n)] = dsw_new
-            nc.vector.tensor_copy(out=bec(st[("dsw", n)][:])[:, :, 1 - eo, :],
-                                  in_=bec(st[("bank", "e", n)][:])[:, :, eo, :])
+        def copy_den(n):
+            dsw = fin.tile([P, 512], F32, name="dsw")
+            st[("dsw", n)] = dsw
+            nc.vector.tensor_copy(out=dsw[:], in_=st[("bank", "e", n)][:])
 
         def div_pp(n):
             first, size = group_of(n)
@@ -277,7 +276,7 @@ def tile_multidimensinalgrucell_pb_t_kernel(
             c0 = (n - first) * 256
             nc.vector.tensor_tensor(out=st[("pp", first)][:, c0:c0 + 256].rearrange("p (b c) -> p b c", b=2),
                                     in0=bec(st[("bank", "e", n)][:])[:, :, 0, :],
-                                    in1=bec(st[("dsw", n)][:])[:, :, 0, :],
+                                    in1=bec(st[("dsw", n)][:])[:, :, 1, :],
                                     op=ALU.mult)
 
         def group_of(n):
@@ -346,17 +345,18 @@ def tile_multidimensinalgrucell_pb_t_kernel(
         evac_b(0)
 
         def den_slot(k):
-            return min(k + LD, max(k + 1, k // 2 + N_PAIRS))
+            return min(k + 3, max(k + 1, k // 2 + N_PAIRS + 1))
 
         def num_slot(k):
-            return min(k + LD + 1, max(k + 2, k // 2 + N_PAIRS + 1))
+            return min(k + 4, max(k + 2, k // 2 + N_PAIRS + 2))
 
-        END = HALVES + 4
+        END = HALVES + 5
+        last = N_PAIRS - 1
         ln_at, exp_at = {}, {}
         outs = {h: [] for h in range(END + 20)}
         for first, size in LOG_GROUPS:
             s = den_slot(2 * (first + size) - 1) + 2
-            if first + size == N_PAIRS - 1:
+            if first + size == last:
                 ln_at[HALVES] = (first, size)
                 exp_at[HALVES] = (first, size)
                 outs[END - 1] += list(range(first, first + size))
@@ -366,71 +366,74 @@ def tile_multidimensinalgrucell_pb_t_kernel(
             for i in range(size):
                 o = s + 4 + i
                 outs[o if o < HALVES - 3 else HALVES + 1].append(first + i)
-        last = N_PAIRS - 1
         outs[END - 2].append(last)
         for h in range(END):
             n, eo = divmod(h, 2)
+            nq, tq = divmod(h + 5, 2)
+            after_ln = any(0 < h - s <= 3 for s in ln_at)
+            here = [q for q in range(N_PAIRS) if den_slot(2 * q + 1) + 1 == h]
+            num_done = [q for q in range(N_PAIRS) if num_slot(2 * q + 1) + 1 == h]
             if eo == 0 and ok(n + 5):
                 load(n + 5)
+            if h < HALVES:
+                maximum(h, 1)
+            if h == 0:
+                quant_w(1, 0)
+            for q in here:
+                copy_den(q)
+            if 0 <= h - 1 < HALVES:
+                shift(h - 1, 0)
             if 0 < h < HALVES - 1:
                 mx(h + 1, 0)
-            after_ln = any(0 < h - s <= 3 for s in ln_at)
-            nq, tq = divmod(h + 5, 2)
-            if ok(nq):
-                in_q(nq, tq)
-            if after_ln:
-                if h + 1 < HALVES:
-                    first_gate(h + 1)
-                if ok(nq):
-                    evac_q(nq, tq)
-            if 1 <= h <= HALVES:
-                exps(h - 1)
-                products(h - 1, nc.gpsimd)
-            fill = []
-            for q in range(N_PAIRS):
-                if num_slot(2 * q + 1) + 1 == h:
-                    fill.append((div_cr, q))
-            for k in range(HALVES):
-                if den_slot(k) + 1 == h:
-                    fill.append((swap_den, k))
-                    if k % 2:
-                        fill.append((div_pp, k // 2))
-                        if k // 2 == last:
-                            fill.append((lambda q: (div_r(q, 0), div_r(q, 1)), k // 2))
-            if h == 0:
-                fill = [(lambda q: quant_w(1, 0), 0), (lambda q: quant_w(1, 1), 0), (quant, 1)]
-            elif eo == 0 and ok(n + 1):
-                quant(n + 1)
-            for j in range(1, 4):
-                if h < HALVES:
-                    maximum(h, j)
-                if fill:
-                    f, arg = fill.pop(0)
-                    f(arg)
+            for q in here:
+                div_pp(q)
+            if not after_ln and 0 <= h - 1 < HALVES:
+                exps(h - 1, 0)
+            ne, te = divmod(h + 4, 2)
+            if h > 0 and ok(ne):
+                evac_q(ne, te)
             if h < HALVES:
-                shifts(h)
+                maximum(h, 2)
             if h == 0:
+                quant_w(1, 1)
                 mx(1, 0)
-            for f, arg in fill:
-                f(arg)
-            for m in outs[h]:
-                div_out(m, nc.vector if h >= HALVES else nc.gpsimd)
+                mx(1, 1)
+            if h + 1 < HALVES:
+                first_gate(h + 1)
+            if 0 <= h - 1 < HALVES:
+                shift(h - 1, 1)
+            if h < HALVES:
+                maximum(h, 3)
+            if eo == 1 and ok(n + 1):
+                in_b(n + 1)
+            if h < HALVES:
+                for k in range(HALVES):
+                    if den_slot(k) == h:
+                        sum_t("e", k)
+            for q in num_done:
+                div_cr(q)
+            if 0 < h < HALVES - 1:
+                mx(h + 1, 1)
+            if 0 <= h - 1 < HALVES:
+                if after_ln:
+                    exps(h - 1, 0)
+                exps(h - 1, 1)
+                products(h - 1, nc.gpsimd)
             if h >= HALVES:
                 for k in range(HALVES):
                     if den_slot(k) == h:
                         sum_t("e", k)
-            for k in range(HALVES):
-                if num_slot(k) == h:
-                    sum_t("pr", k)
-            if not after_ln:
-                if h + 1 < HALVES:
-                    first_gate(h + 1)
-                if ok(nq):
-                    evac_q(nq, tq)
-            if h + 1 < HALVES:
-                mx(h + 1, 1)
+            if eo == 0 and ok(n + 1):
+                quant(n + 1)
+            for q in here:
+                if q == last:
+                    div_r(q, 0)
+                    div_r(q, 1)
+            for m in outs[h]:
+                div_out(m, nc.vector if h >= HALVES else nc.gpsimd)
+            if ok(nq):
+                in_q(nq, tq)
             if eo == 1 and ok(n + 1):
-                in_b(n + 1)
                 evac_b(n + 1)
             if h in ln_at:
                 group_ln(*ln_at[h])
@@ -440,7 +443,6 @@ def tile_multidimensinalgrucell_pb_t_kernel(
                 else:
                     for m in range(exp_at[h][1]):
                         group_exp(exp_at[h][0], 1, m)
-            if h < HALVES:
-                for k in range(HALVES):
-                    if den_slot(k) == h:
-                        sum_t("e", k)
+            for k in range(HALVES):
+                if num_slot(k) == h:
+                    sum_t("pr", k)

@@ -178,7 +178,6 @@ def tile_multidimensinalgrucell_pb_t_kernel(
             qc, qs = st[("q", n)]
             bank = ps.tile([P, 512], F32, name="l%d%d" % (g, eo))
             st[("l", h, g)] = bank
-            nc.tensor.matmul(out=bank[:, 0:KEEP], lhsT=spare[:, 0:128], rhs=spare[:, 0:KEEP], start=True, stop=True)
             for j in range(2 * g, 2 * g + 2):
                 c0 = (j % 2) * 256
                 for s in range(2):
@@ -341,14 +340,15 @@ def tile_multidimensinalgrucell_pb_t_kernel(
         regroup_w(gp_copy, 1, 3)
         in_q(2, 0)
         evac_q(2, 0)
+        in_q(2, 1)
         in_b(0)
         evac_b(0)
 
         def den_slot(k):
-            return min(k + 3, max(k + 1, k // 2 + N_PAIRS + 1))
+            return min(k + 2, max(k + 1, k // 2 + N_PAIRS + 1))
 
         def num_slot(k):
-            return min(k + 4, max(k + 2, k // 2 + N_PAIRS + 2))
+            return min(k + 3, max(k + 2, k // 2 + N_PAIRS + 2))
 
         END = HALVES + 5
         last = N_PAIRS - 1
@@ -369,72 +369,66 @@ def tile_multidimensinalgrucell_pb_t_kernel(
         outs[END - 2].append(last)
         for h in range(END):
             n, eo = divmod(h, 2)
-            nq, tq = divmod(h + 5, 2)
+            nq, tq = divmod(h + 6, 2)
+            ne, te = divmod(h + 5, 2)
             after_ln = any(0 < h - s <= 3 for s in ln_at)
-            here = [q for q in range(N_PAIRS) if den_slot(2 * q + 1) + 1 == h]
+            den_done = [q for q in range(N_PAIRS) if den_slot(2 * q + 1) + 1 == h]
             num_done = [q for q in range(N_PAIRS) if num_slot(2 * q + 1) + 1 == h]
             if eo == 0 and ok(n + 5):
                 load(n + 5)
-            if h < HALVES:
-                maximum(h, 1)
-            if h == 0:
-                quant_w(1, 0)
-            for q in here:
-                copy_den(q)
             if 0 <= h - 1 < HALVES:
                 shift(h - 1, 0)
-            if 0 < h < HALVES - 1:
-                mx(h + 1, 0)
-            for q in here:
-                div_pp(q)
-            if not after_ln and 0 <= h - 1 < HALVES:
-                exps(h - 1, 0)
-            ne, te = divmod(h + 4, 2)
-            if h > 0 and ok(ne):
+                if not after_ln:
+                    exps(h - 1, 0)
+            if h < HALVES:
+                maximum(h, 1)
+            if 0 <= h - 1 < HALVES:
+                shift(h - 1, 1)
+                if not after_ln:
+                    exps(h - 1, 1)
+            if ok(ne):
                 evac_q(ne, te)
             if h < HALVES:
                 maximum(h, 2)
             if h == 0:
-                quant_w(1, 1)
-                mx(1, 0)
-                mx(1, 1)
-            if h + 1 < HALVES:
-                first_gate(h + 1)
-            if 0 <= h - 1 < HALVES:
-                shift(h - 1, 1)
-            if h < HALVES:
-                maximum(h, 3)
-            if eo == 1 and ok(n + 1):
-                in_b(n + 1)
-            if h < HALVES:
-                for k in range(HALVES):
-                    if den_slot(k) == h:
-                        sum_t("e", k)
+                quant_w(1, 0)
+            for q in den_done:
+                copy_den(q)
             for q in num_done:
                 div_cr(q)
-            if 0 < h < HALVES - 1:
+            if h < HALVES:
+                maximum(h, 3)
+            if h == 0:
+                quant_w(1, 1)
+                quant(1)
+            if h + 1 < HALVES:
+                mx(h + 1, 0)
                 mx(h + 1, 1)
-            if 0 <= h - 1 < HALVES:
-                if after_ln:
-                    exps(h - 1, 0)
+                first_gate(h + 1)
+            if after_ln and h - 1 < HALVES:
+                exps(h - 1, 0)
                 exps(h - 1, 1)
+            if 0 <= h - 1 < HALVES:
                 products(h - 1, nc.gpsimd)
-            if h >= HALVES:
-                for k in range(HALVES):
-                    if den_slot(k) == h:
-                        sum_t("e", k)
-            if eo == 0 and ok(n + 1):
-                quant(n + 1)
-            for q in here:
+            for q in den_done:
+                div_pp(q)
+            if eo == 1 and ok(n + 2):
+                quant(n + 2)
+            for q in den_done:
                 if q == last:
                     div_r(q, 0)
                     div_r(q, 1)
             for m in outs[h]:
                 div_out(m, nc.vector if h >= HALVES else nc.gpsimd)
+            if eo == 1 and ok(n + 1):
+                in_b(n + 1)
+                evac_b(n + 1)
+            if h < HALVES:
+                for k in range(HALVES):
+                    if num_slot(k) == h:
+                        sum_t("pr", k)
             if ok(nq):
                 in_q(nq, tq)
-            if eo == 1 and ok(n + 1):
-                evac_b(n + 1)
             if h in ln_at:
                 group_ln(*ln_at[h])
             if h in exp_at:
@@ -444,5 +438,9 @@ def tile_multidimensinalgrucell_pb_t_kernel(
                     for m in range(exp_at[h][1]):
                         group_exp(exp_at[h][0], 1, m)
             for k in range(HALVES):
-                if num_slot(k) == h:
-                    sum_t("pr", k)
+                if den_slot(k) == h:
+                    sum_t("e", k)
+            if h >= HALVES:
+                for k in range(HALVES):
+                    if num_slot(k) == h:
+                        sum_t("pr", k)

@@ -47,7 +47,7 @@ def tile_multidimensinalgrucell_pb_t_kernel(
         soft = ctx.enter_context(tc.tile_pool(name="soft", bufs=3))
         deep = ctx.enter_context(tc.tile_pool(name="deep", bufs=6))
         grpd = ctx.enter_context(tc.tile_pool(name="grpd", bufs=2))
-        stor = ctx.enter_context(tc.tile_pool(name="stor", bufs=4))
+        stor = ctx.enter_context(tc.tile_pool(name="stor", bufs=6))
         late = ctx.enter_context(tc.tile_pool(name="late", bufs=8))
         fin = ctx.enter_context(tc.tile_pool(name="fin", bufs=3))
         ps = ctx.enter_context(tc.psum_pool(name="ps", bufs=1))
@@ -73,7 +73,7 @@ def tile_multidimensinalgrucell_pb_t_kernel(
 
         ident = const.tile([P, P], F32, name="ident")
         make_identity(nc, ident[:])
-        spare = const.tile([P, 256], BF16, name="spare")
+        spare = const.tile([P, 512], BF16, name="spare")
         nc.gpsimd.memset(spare[:], 0.0)
         brow = const.tile([P, 256], BF16, name="brow")
         nc.vector.memset(brow[:], 0.0)
@@ -178,6 +178,7 @@ def tile_multidimensinalgrucell_pb_t_kernel(
             qc, qs = st[("q", n)]
             bank = ps.tile([P, 512], F32, name="l%d%d" % (g, eo))
             st[("l", h, g)] = bank
+            nc.tensor.matmul(out=bank[:, 0:KEEP], lhsT=spare[:, 0:128], rhs=spare[:, 0:KEEP], start=True, stop=True)
             for j in range(2 * g, 2 * g + 2):
                 c0 = (j % 2) * 256
                 for s in range(2):
@@ -345,10 +346,10 @@ def tile_multidimensinalgrucell_pb_t_kernel(
         evac_b(0)
 
         def den_slot(k):
-            return min(k + 2, max(k + 1, k // 2 + N_PAIRS + 1))
+            return min(k + 3, max(k + 1, k // 2 + N_PAIRS + 1))
 
         def num_slot(k):
-            return min(k + 3, max(k + 2, k // 2 + N_PAIRS + 2))
+            return min(k + 4, max(k + 2, k // 2 + N_PAIRS + 2))
 
         END = HALVES + 5
         last = N_PAIRS - 1
@@ -371,22 +372,32 @@ def tile_multidimensinalgrucell_pb_t_kernel(
             n, eo = divmod(h, 2)
             nq, tq = divmod(h + 6, 2)
             ne, te = divmod(h + 5, 2)
-            after_ln = any(0 < h - s <= 3 for s in ln_at)
+            after_ln = any(0 < h - s <= 4 for s in ln_at)
             den_done = [q for q in range(N_PAIRS) if den_slot(2 * q + 1) + 1 == h]
             num_done = [q for q in range(N_PAIRS) if num_slot(2 * q + 1) + 1 == h]
             if eo == 0 and ok(n + 5):
                 load(n + 5)
+            if ok(ne) and not after_ln:
+                evac_q(ne, te)
             if 0 <= h - 1 < HALVES:
                 shift(h - 1, 0)
                 if not after_ln:
                     exps(h - 1, 0)
+            if 0 < h < HALVES - 1:
+                mx(h + 1, 0)
+            early = [("e", k) for k in range(1, HALVES, 2) if den_slot(k - 1) < den_slot(k) == h < HALVES]
+            early += [("pr", k) for k in range(1, HALVES, 2) if num_slot(k - 1) < num_slot(k) == h < HALVES]
+            for key, k in early:
+                sum_t(key, k)
             if h < HALVES:
                 maximum(h, 1)
             if 0 <= h - 1 < HALVES:
                 shift(h - 1, 1)
                 if not after_ln:
                     exps(h - 1, 1)
-            if ok(ne):
+            if 0 < h < HALVES - 1:
+                first_gate(h + 1)
+            if ok(ne) and after_ln:
                 evac_q(ne, te)
             if h < HALVES:
                 maximum(h, 2)
@@ -401,10 +412,11 @@ def tile_multidimensinalgrucell_pb_t_kernel(
             if h == 0:
                 quant_w(1, 1)
                 quant(1)
+            if h == 0:
+                mx(1, 0)
+                first_gate(1)
             if h + 1 < HALVES:
-                mx(h + 1, 0)
                 mx(h + 1, 1)
-                first_gate(h + 1)
             if after_ln and h - 1 < HALVES:
                 exps(h - 1, 0)
                 exps(h - 1, 1)
@@ -412,8 +424,8 @@ def tile_multidimensinalgrucell_pb_t_kernel(
                 products(h - 1, nc.gpsimd)
             for q in den_done:
                 div_pp(q)
-            if eo == 1 and ok(n + 2):
-                quant(n + 2)
+            if eo == 0 and h > 0 and ok(n + 1):
+                quant(n + 1)
             for q in den_done:
                 if q == last:
                     div_r(q, 0)
@@ -423,10 +435,6 @@ def tile_multidimensinalgrucell_pb_t_kernel(
             if eo == 1 and ok(n + 1):
                 in_b(n + 1)
                 evac_b(n + 1)
-            if h < HALVES:
-                for k in range(HALVES):
-                    if num_slot(k) == h:
-                        sum_t("pr", k)
             if ok(nq):
                 in_q(nq, tq)
             if h in ln_at:
@@ -438,9 +446,8 @@ def tile_multidimensinalgrucell_pb_t_kernel(
                     for m in range(exp_at[h][1]):
                         group_exp(exp_at[h][0], 1, m)
             for k in range(HALVES):
-                if den_slot(k) == h:
+                if den_slot(k) == h and ("e", k) not in early:
                     sum_t("e", k)
-            if h >= HALVES:
-                for k in range(HALVES):
-                    if num_slot(k) == h:
-                        sum_t("pr", k)
+            for k in range(HALVES):
+                if num_slot(k) == h and ("pr", k) not in early:
+                    sum_t("pr", k)

from contextlib import ExitStack

import concourse.mybir as mybir
from concourse.masks import make_identity

F32 = mybir.dt.float32
BF16 = mybir.dt.bfloat16
U32 = mybir.dt.uint32
U8 = mybir.dt.uint8
FP8X4 = mybir.dt.float8_e4m3fn_x4
ACT = mybir.ActivationFunctionType
ALU = mybir.AluOpType

P = 128
KEEP = 128
BATCH = 4096
UNITS = 256
N_PAIRS = 16
LOG_GROUPS = ((0, 4), (4, 4), (8, 4), (12, 3))
LD = 3
HALVES = 2 * N_PAIRS
FLOPS = 2 * BATCH * 1024 * 1024


def tile_multidimensinalgrucell_pb_t_kernel(
    tc, x, left_state, top_state, diagonal_state, h_cand,
    w_zi, b_zi, w_zl, b_zl, w_zt, b_zt, w_zd, b_zd, out,
):
    nc = tc.nc
    gate_w = [w_zl, w_zt, w_zd, w_zi]
    gate_b = [b_zl, b_zt, b_zd, b_zi]

    def rows(a):
        return a.rearrange("(p n t) f -> p n (t f)", n=N_PAIRS, t=2)

    def rows3(a):
        return a.rearrange("(p n t) (a f) -> p n (t a) f", n=N_PAIRS, t=2, a=2)

    left_v, top_v, h_v, out_v = rows(left_state), rows(top_state), rows(h_cand), rows(out)
    diag_v, x_v, dg_v = rows3(diagonal_state), rows3(x), rows(diagonal_state)

    with ExitStack() as ctx:
        const = ctx.enter_context(tc.tile_pool(name="const", bufs=1))
        inp = ctx.enter_context(tc.tile_pool(name="inp", bufs=6))
        grp = ctx.enter_context(tc.tile_pool(name="grp", bufs=5))
        qnt = ctx.enter_context(tc.tile_pool(name="qnt", bufs=2))
        soft = ctx.enter_context(tc.tile_pool(name="soft", bufs=3))
        deep = ctx.enter_context(tc.tile_pool(name="deep", bufs=6))
        grpd = ctx.enter_context(tc.tile_pool(name="grpd", bufs=2))
        stor = ctx.enter_context(tc.tile_pool(name="stor", bufs=6))
        late = ctx.enter_context(tc.tile_pool(name="late", bufs=8))
        fin = ctx.enter_context(tc.tile_pool(name="fin", bufs=3))
        ps = ctx.enter_context(tc.psum_pool(name="ps", bufs=1))
        ps2 = ctx.enter_context(tc.psum_pool(name="ps2", bufs=2))
        ctx.enter_context(tc.manual_schedule())

        st = {}

        def load(n):
            lf = inp.tile([P, 512], BF16, name="lf")
            tp = inp.tile([P, 512], BF16, name="tp")
            dx = inp.tile([P, 1024], BF16, name="dx")
            dg = inp.tile([P, 512], BF16, name="dg")
            hc = inp.tile([P, 512], BF16, name="hc")
            dx4 = dx[:].rearrange("p (y s f) -> p y s f", y=4, s=2)
            nc.sync.dma_start(out=lf[:], in_=left_v[:, n, :])
            nc.sync.dma_start(out=tp[:], in_=top_v[:, n, :])
            nc.sync.dma_start(out=dx4[:, :, 0, :], in_=diag_v[:, n])
            nc.sync.dma_start(out=dx4[:, :, 1, :], in_=x_v[:, n])
            nc.sync.dma_start(out=hc[:], in_=h_v[:, n, :])
            nc.sync.dma_start(out=dg[:], in_=dg_v[:, n, :])
            st[("in", n)] = (lf, tp, dx, hc, dg)

        ident = const.tile([P, P], F32, name="ident")
        make_identity(nc, ident[:])
        spare = const.tile([P, 512], BF16, name="spare")
        nc.gpsimd.memset(spare[:], 0.0)
        brow = const.tile([P, 256], BF16, name="brow")
        nc.vector.memset(brow[:], 0.0)
        warm = const.tile([P, 8], F32, name="warm")
        nc.vector.memset(warm[:], 0.0)
        nc.scalar.activation(out=warm[:], in_=warm[:], func=ACT.Exp)
        for j in range(4):
            nc.scalar.dma_start(out=brow[j:j + 1, :], in_=gate_b[j].rearrange("(o f) -> o f", o=1))
        load(0)
        wraw = const.tile([P, 8192], BF16, name="wraw")
        for j in range(4):
            nc.sync.dma_start(
                out=wraw[:, j * 2048:j * 2048 + 1024].rearrange("p (u y) -> p u y", u=2),
                in_=gate_w[j][0:512, :].rearrange("(u p e) c -> p u (e c)", u=2, e=2),
            )
            for g in range(2):
                nc.sync.dma_start(
                    out=wraw[g * 64:(g + 1) * 64, j * 2048 + 1024:(j + 1) * 2048].rearrange("p (u y) -> p u y", u=2),
                    in_=gate_w[j][512 + g * 256:768 + g * 256, :].rearrange("(u p e) c -> p u (e c)", u=2, e=2),
                )
        load(1)
        load(2)
        load(3)
        load(4)

        tb0 = ps2.tile([P, 512], F32, name="tr")
        nc.tensor.transpose(tb0[:, 0:128], brow[:].bitcast(F32), ident[:])
        bw = const.tile([P, 4], F32, name="bw")
        nc.vector.tensor_copy(out=bw[:], in_=tb0[:, 0:4])
        bcol = const.tile([P, 8], F32, name="bcol")
        nc.vector.tensor_copy(out=bcol[:], in_=bw[:].bitcast(BF16))

        wg = const.tile([P, 8192], BF16, name="wg", align_bytes=64)
        wc = const.tile([P, 2048], U32, name="wc", align_bytes=64)
        ws = const.tile([P, 2048], U8, name="ws", align_bytes=64)
        wg6 = wg[:].rearrange("p (e j s c t) -> p e j s c t", e=2, j=4, s=2, t=4)

        def regroup_w(eng_copy, eo, j):
            src = wraw[:, j * 2048:(j + 1) * 2048].rearrange(
                "p (s t c e) -> p e s c t", s=2, t=4, e=2)
            eng_copy(out=wg6[:, eo, j], in_=src[:, eo])

        def quant_w(eo, jp):
            g0 = eo * 4 + jp * 2
            nc.vector.quantize_mx(
                out=wc[:, g0 * 256:(g0 + 2) * 256].bitcast(FP8X4),
                scales=ws[:, g0 * 256:(g0 + 2) * 256],
                in_=wg[:, g0 * 1024:(g0 + 2) * 1024],
            )

        def gp_copy(out, in_):
            nc.gpsimd.tensor_scalar(out=out, in0=in_, scalar1=1.0, scalar2=0.0, op0=ALU.mult, op1=ALU.add)

        def in_q(n, tl):
            lf, tp, dx, hc, dg = st[("in", n)]
            tr = ps2.tile([P, 512], F32, name="tr")
            lfw, tpw, dxw = [a[:].bitcast(F32) for a in (lf, tp, dx)]
            w0 = tl * 128
            d0 = tl * 256
            nc.tensor.transpose(tr[:, 0:128], lfw[:, w0:w0 + 128], ident[:])
            nc.tensor.transpose(tr[:, 128:256], tpw[:, w0:w0 + 128], ident[:])
            nc.tensor.transpose(tr[:, 256:384], dxw[:, d0:d0 + 128], ident[:])
            nc.tensor.transpose(tr[:, 384:512], dxw[:, d0 + 128:d0 + 256], ident[:])
            st[("tr", n, tl)] = tr

        def evac_q(n, tl):
            if tl == 0:
                gq_new = grp.tile([P, 2048], BF16, name="gq", align_bytes=64)
                st[("gq", n)] = gq_new
            c0 = tl * 128
            nc.scalar.copy(
                out=st[("gq", n)][:].bitcast(F32).rearrange("p (s c u) -> p s c u", s=2, u=2)[:, :, c0:c0 + 128, :],
                in_=st[("tr", n, tl)][:].rearrange("p (s u r) -> p s r u", s=2, u=2),
            )

        def in_b(n):
            lf, tp, dx, hc, dg = st[("in", n)]
            tb = ps2.tile([P, 512], F32, name="tr")
            dgw, hcw = [a[:].bitcast(F32) for a in (dg, hc)]
            for tl in range(2):
                nc.tensor.transpose(tb[:, tl * 128:tl * 128 + 128], dgw[:, tl * 128:tl * 128 + 128], ident[:])
            for tl in range(2):
                nc.tensor.transpose(tb[:, 256 + tl * 128:384 + tl * 128], hcw[:, tl * 128:tl * 128 + 128], ident[:])
            st[("tb", n)] = tb

        def evac_b(n):
            gb = grp.tile([P, 1024], BF16, name="gb", align_bytes=64)
            st[("gb", n)] = gb
            nc.scalar.copy(
                out=gb[:].bitcast(F32).rearrange("p (c s) -> p c s", s=2),
                in_=st[("tb", n)][:].rearrange("p (s c) -> p c s", s=2),
            )

        def quant(n):
            qc = qnt.tile([P, 512], U32, name="qc", align_bytes=64)
            qs = qnt.tile([P, 512], U8, name="qs", align_bytes=64)
            nc.vector.quantize_mx(out=qc[:].bitcast(FP8X4), scales=qs[:], in_=st[("gq", n)][:])
            st[("q", n)] = (qc, qs)

        def mx(h, g):
            n, eo = divmod(h, 2)
            qc, qs = st[("q", n)]
            bank = ps.tile([P, 512], F32, name="l%d%d" % (g, eo))
            st[("l", h, g)] = bank
            nc.tensor.matmul(out=bank[:, 0:KEEP], lhsT=spare[:, 0:128], rhs=spare[:, 0:KEEP], start=True, stop=True)
            for j in range(2 * g, 2 * g + 2):
                c0 = (j % 2) * 256
                for s in range(2):
                    b0 = ((eo * 4 + j) * 2 + s) * 128
                    nc.tensor.matmul_mx(
                        out=bank[:, c0:c0 + 256],
                        lhsT=wc[:, b0:b0 + 128].bitcast(FP8X4),
                        lhsT_scale=ws[:, b0:b0 + 128],
                        rhs=qc[:, s * 256:(s + 1) * 256].bitcast(FP8X4),
                        rhs_scale=qs[:, s * 256:(s + 1) * 256],
                        start=(s == 0),
                        stop=(s == 1),
                    )

        def logit(h, j):
            return st[("l", h, j // 2)][:, (j % 2) * 256:(j % 2) * 256 + 256]

        def bias(h, j):
            return bcol[:, 2 * j + h % 2:2 * j + h % 2 + 1]

        def first_gate(h):
            a0 = soft.tile([P, 256], F32, name="a0")
            nc.scalar.activation(out=a0[:], in_=logit(h, 0), func=ACT.Identity, bias=bias(h, 0), scale=1.0)
            st[("m", h)] = a0

        def maximum(h, j):
            m = soft.tile([P, 256], F32, name="m%d" % j)
            nc.vector.scalar_tensor_tensor(
                out=m[:], in0=logit(h, j), scalar=bias(h, j), in1=st[("m", h)][:],
                op0=ALU.add, op1=ALU.max)
            st[("m", h)] = m

        def shift(h, g):
            if g == 0:
                e_new = deep.tile([P, 1024], F32, name="e")
                st[("e", h)] = e_new
            nc.vector.tensor_tensor(
                out=st[("e", h)][:, g * 512:(g + 1) * 512].rearrange("p (j c) -> p j c", j=2),
                in0=st[("l", h, g)][:].rearrange("p (j c) -> p j c", j=2),
                in1=st[("m", h)][:].unsqueeze(1).to_broadcast([P, 2, 256]),
                op=ALU.subtract)

        def exps(h, g):
            e = st[("e", h)]
            for j in range(2 * g, 2 * g + 2):
                nc.scalar.activation(out=e[:, j * 256:(j + 1) * 256], in_=e[:, j * 256:(j + 1) * 256],
                                     func=ACT.Exp, bias=bias(h, j), scale=1.0)

        def products(h, eng):
            n, eo = divmod(h, 2)
            e = st[("e", h)]
            pr = deep.tile([P, 1024], F32, name="pr")
            st[("pr", h)] = pr
            for half, src in ((0, st[("gq", n)][:, 0:1024]), (1, st[("gb", n)][:])):
                sv = src.rearrange("p (c u e) -> p u e c", u=2, e=2)[:, :, eo, :]
                eng.tensor_tensor(
                    out=pr[:, half * 512:(half + 1) * 512].rearrange("p (u c) -> p u c", u=2),
                    in0=e[:, half * 512:(half + 1) * 512].rearrange("p (u c) -> p u c", u=2),
                    in1=sv, op=ALU.mult)

        def sum_t(key, h):
            n, eo = divmod(h, 2)
            if eo == 0:
                bank_new = ps.tile([P, 512], F32, name="bank_" + key)
                st[("bank", key, n)] = bank_new
            bank = st[("bank", key, n)]
            src = st[(key, h)]
            for blk in range(2):
                c0 = blk * 256 + (1 - eo if key == "e" else eo) * 128
                for j in range(4):
                    nc.tensor.matmul(
                        out=bank[:, c0:c0 + 128],
                        lhsT=src[:, j * 256 + blk * 128:j * 256 + blk * 128 + 128],
                        rhs=ident[:], is_transpose=True,
                        start=(j == 0), stop=(j == 3))

        def bec(ap):
            return ap.rearrange("p (b e c) -> p b e c", b=2, e=2)

        def copy_den(n):
            dsw = fin.tile([P, 512], F32, name="dsw")
            st[("dsw", n)] = dsw
            nc.vector.tensor_copy(out=dsw[:], in_=st[("bank", "e", n)][:])

        def div_pp(n):
            first, size = group_of(n)
            if size == 1:
                pp_one = fin.tile([P, 256], F32, name="pp_one")
                rr_one = fin.tile([P, 256], F32, name="rr_one")
                st[("pp", n)], st[("rr", n)] = pp_one, rr_one
            elif n == first:
                pp_new = grpd.tile([P, 1024], F32, name="pp")
                rr_new = grpd.tile([P, 1024], F32, name="rr")
                st[("pp", first)], st[("rr", first)] = pp_new, rr_new
            c0 = (n - first) * 256
            nc.vector.tensor_tensor(out=st[("pp", first)][:, c0:c0 + 256].rearrange("p (b c) -> p b c", b=2),
                                    in0=bec(st[("bank", "e", n)][:])[:, :, 0, :],
                                    in1=bec(st[("dsw", n)][:])[:, :, 1, :],
                                    op=ALU.mult)

        def group_of(n):
            for first, size in LOG_GROUPS:
                if first <= n < first + size:
                    return first, size
            return n, 1

        def group_ln(first, size):
            pp = st[("pp", first)]
            nc.scalar.activation(out=pp[:, 0:size * 256], in_=pp[:, 0:size * 256], func=ACT.Ln)

        def group_exp(first, size, skip=0):
            a, b = skip * 256, (skip + size) * 256
            nc.scalar.activation(out=st[("rr", first)][:, a:b], in_=st[("pp", first)][:, a:b],
                                 func=ACT.Exp, scale=-1.0)

        def div_cr(n):
            cr = late.tile([P, 512], F32, name="cr")
            st[("cr", n)] = cr
            nc.vector.tensor_tensor(out=cr[:], in0=st[("bank", "pr", n)][:], in1=st[("dsw", n)][:], op=ALU.mult)

        def div_r(n, b):
            nc.vector.reciprocal(out=st[("rr", n)][:, b * 128:b * 128 + 128],
                                 in_=st[("pp", n)][:, b * 128:b * 128 + 128])

        def div_out(n, eng):
            first, size = group_of(n)
            r0 = (n - first) * 256
            osb = stor.tile([P, 512], F32, name="osb")
            eng.tensor_tensor(
                out=osb[:].rearrange("p (b c e) -> p b c e", b=2, e=2),
                in0=st[("cr", n)][:].rearrange("p (b e c) -> p b c e", b=2, e=2),
                in1=st[("rr", first)][:, r0:r0 + 256].rearrange("p (b c) -> p b c", b=2).unsqueeze(3).to_broadcast([P, 2, 128, 2]),
                op=ALU.mult)
            nc.sync.dma_start(out=out_v[:, n, :], in_=osb[:])

        def ok(n):
            return 0 <= n < N_PAIRS

        in_q(0, 0)
        evac_q(0, 0)
        in_q(0, 1)
        evac_q(0, 1)
        regroup_w(nc.vector.tensor_copy, 0, 0)
        regroup_w(nc.vector.tensor_copy, 0, 1)
        quant(0)
        quant_w(0, 0)
        regroup_w(nc.scalar.copy, 1, 0)
        regroup_w(nc.scalar.copy, 1, 1)
        in_q(1, 0)
        mx(0, 0)
        first_gate(0)
        evac_q(1, 0)
        regroup_w(nc.vector.tensor_copy, 0, 2)
        regroup_w(nc.vector.tensor_copy, 0, 3)
        quant_w(0, 1)
        in_q(1, 1)
        mx(0, 1)
        evac_q(1, 1)
        regroup_w(nc.scalar.copy, 1, 2)
        regroup_w(gp_copy, 1, 3)
        in_q(2, 0)
        evac_q(2, 0)
        in_q(2, 1)
        in_b(0)
        evac_b(0)

        def den_slot(k):
            return min(k + 3, max(k + 1, k // 2 + N_PAIRS + 1))

        def num_slot(k):
            return min(k + 4, max(k + 2, k // 2 + N_PAIRS + 2))

        END = HALVES + 5
        last = N_PAIRS - 1
        ln_at, exp_at = {}, {}
        outs = {h: [] for h in range(END + 20)}
        for first, size in LOG_GROUPS:
            s = den_slot(2 * (first + size) - 1) + 2
            if first + size == last:
                ln_at[HALVES] = (first, size)
                exp_at[HALVES] = (first, size)
                outs[END - 1] += list(range(first, first + size))
                continue
            ln_at[s] = (first, size)
            exp_at[s + 3] = (first, size)
            for i in range(size):
                o = s + 4 + i
                outs[o if o < HALVES - 3 else HALVES + 1].append(first + i)
        outs[END - 2].append(last)
        for h in range(END):
            n, eo = divmod(h, 2)
            nq, tq = divmod(h + 6, 2)
            ne, te = divmod(h + 5, 2)
            after_ln = any(0 < h - s <= 4 for s in ln_at)
            den_done = [q for q in range(N_PAIRS) if den_slot(2 * q + 1) + 1 == h]
            num_done = [q for q in range(N_PAIRS) if num_slot(2 * q + 1) + 1 == h]
            if eo == 0 and ok(n + 5):
                load(n + 5)
            if ok(ne) and not after_ln:
                evac_q(ne, te)
            if 0 <= h - 1 < HALVES:
                shift(h - 1, 0)
                if not after_ln:
                    exps(h - 1, 0)
            if 0 < h < HALVES - 1:
                mx(h + 1, 0)
            early = [("e", k) for k in range(1, HALVES, 2) if den_slot(k - 1) < den_slot(k) == h < HALVES]
            early += [("pr", k) for k in range(1, HALVES, 2) if num_slot(k - 1) < num_slot(k) == h < HALVES]
            for key, k in early:
                sum_t(key, k)
            if h < HALVES:
                maximum(h, 1)
            if 0 <= h - 1 < HALVES:
                shift(h - 1, 1)
                if not after_ln:
                    exps(h - 1, 1)
            if 0 < h < HALVES - 1:
                first_gate(h + 1)
            if ok(ne) and after_ln:
                evac_q(ne, te)
            if h < HALVES:
                maximum(h, 2)
            if h == 0:
                quant_w(1, 0)
            for q in den_done:
                copy_den(q)
            for q in num_done:
                div_cr(q)
            if h < HALVES:
                maximum(h, 3)
            if h == 0:
                quant_w(1, 1)
                quant(1)
            if h == 0:
                mx(1, 0)
                first_gate(1)
            if h + 1 < HALVES:
                mx(h + 1, 1)
            if after_ln and h - 1 < HALVES:
                exps(h - 1, 0)
                exps(h - 1, 1)
            if 0 <= h - 1 < HALVES:
                products(h - 1, nc.gpsimd)
            for q in den_done:
                div_pp(q)
            if eo == 0 and h > 0 and ok(n + 1):
                quant(n + 1)
            for q in den_done:
                if q == last:
                    div_r(q, 0)
                    div_r(q, 1)
            for m in outs[h]:
                div_out(m, nc.vector if h >= HALVES else nc.gpsimd)
            if eo == 1 and ok(n + 1):
                in_b(n + 1)
                evac_b(n + 1)
            if ok(nq):
                in_q(nq, tq)
            if h in ln_at:
                group_ln(*ln_at[h])
            if h in exp_at:
                if h < HALVES:
                    group_exp(*exp_at[h])
                else:
                    for m in range(exp_at[h][1]):
                        group_exp(exp_at[h][0], 1, m)
            for k in range(HALVES):
                if den_slot(k) == h and ("e", k) not in early:
                    sum_t("e", k)
            for k in range(HALVES):
                if num_slot(k) == h and ("pr", k) not in early:
                    sum_t("pr", k)
